import numpy as np
import ml_dtypes


def mxq(x, axis, fmt="e4m3"):
    dtype, down = {"e4m3": (ml_dtypes.float8_e4m3fn, 7), "e5m2": (ml_dtypes.float8_e5m2, 14)}[fmt]
    v = np.moveaxis(np.asarray(x, np.float32).astype(ml_dtypes.bfloat16).astype(np.float64), axis, -1)
    blocks = v.reshape(v.shape[:-1] + (-1, 32))
    amax = np.abs(blocks).max(-1, keepdims=True)
    byte = np.maximum(np.where(amax > 0, np.frexp(amax)[1] - 1 + 127, 0) - down, 1)
    scale = np.exp2(byte - 127.0)
    codes = (blocks / scale).astype(np.float32).astype(dtype).astype(np.float64)
    return np.moveaxis((codes * scale).reshape(v.shape), -1, axis)


WIDE = False


def mx_kscale(k):
    if not WIDE:
        return np.ones(k)
    levels = np.array([10, -10, 5, -5, 0])
    a = np.random.permutation(np.resize(levels, k // 512 * 4)).reshape(k // 512, 4)
    idx = np.arange(k)
    return np.exp2(a[idx // 512, idx % 128 // 32])


BF16 = ml_dtypes.bfloat16


def bf(x):
    return np.asarray(x, np.float32).astype(BF16)


def f64(x):
    return np.asarray(x).astype(np.float64)


B, IN, OUT = 4096, 512, 512
G = 3 * OUT


def sigmoid(v):
    return 1.0 / (1.0 + np.exp(-v))


def setup_inputs():
    s = mx_kscale(OUT)
    return {
        "xg": bf(np.random.standard_normal((B, G)) * 0.75),
        "hx": bf(np.random.standard_normal((B, OUT)) * s),
        "cx": bf(np.random.standard_normal((B, OUT))),
        "td0": bf(np.random.uniform(0.0, 1.0, B)),
        "td1": bf(np.random.uniform(0.0, 1.0, B)),
        "w_hh": bf(np.random.standard_normal((G, OUT)) * 0.7 / np.sqrt(OUT) / s),
        "w_pi": bf(np.random.standard_normal((OUT, OUT)) * 0.7 / np.sqrt(OUT)),
        "w_pf": bf(np.random.standard_normal((OUT, OUT)) * 0.7 / np.sqrt(OUT)),
        "b_hh": bf(np.random.standard_normal(G) * 0.3),
        "a": bf(1.0 + 0.1 * np.random.standard_normal(1)),
        "b": bf(0.5 + 0.1 * np.random.standard_normal(1)),
    }


def reference(xg, hx, cx, td0, td1, w_hh, w_pi, w_pf, b_hh, a, b):
    c = f64(cx)
    cq = mxq(c, 1, "e4m3")
    gates = f64(xg) + (mxq(f64(hx), 1, "e4m3") @ mxq(f64(w_hh), 1, "e4m3").T) + f64(b_hh)
    i_g, f_g, g_g = np.split(gates, 3, axis=1)
    i_g = sigmoid(i_g + (cq @ mxq(f64(w_pi), 1, "e4m3").T))
    f_g = sigmoid(f_g + (cq @ mxq(f64(w_pf), 1, "e4m3").T))
    g_g = np.tanh(g_g)
    forcoff = (f64(a) * np.exp(-f64(b) * f64(td0)))[:, None]
    incoff = (f64(a) * np.exp(-f64(b) * f64(td1)))[:, None]
    f_g = forcoff * f_g
    i_g = incoff * i_g
    return f_g * c + i_g * g_g

@@ -1,0 +1,219 @@
+from contextlib import ExitStack
+
+import concourse.mybir as mybir
+from concourse.masks import make_identity
+
+F32 = mybir.dt.float32
+BF16 = mybir.dt.bfloat16
+U32 = mybir.dt.uint32
+U8 = mybir.dt.uint8
+FP8X4 = mybir.dt.float8_e4m3fn_x4
+ALU = mybir.AluOpType
+ACT = mybir.ActivationFunctionType
+
+P = 128
+B = 4096
+K = 512
+OUT = 512
+GATES = 3
+PACK = 4
+HALVES = 2
+SLOTS = B // P
+CHUNK = 4
+N_CHUNKS = SLOTS // CHUNK
+W_TILES = OUT // P
+
+FLOPS = 2 * B * K * (GATES * OUT + 2 * OUT)
+
+
+def tile_ircnn_lstmcell_pa_t_kernel(
+    tc, xg, hx, cx, td0, td1, w_hh, w_pi, w_pf, b_hh, a, b, out
+):
+    nc = tc.nc
+    with ExitStack() as ctx:
+        const = ctx.enter_context(tc.tile_pool(name="const", bufs=1))
+        wstage = ctx.enter_context(tc.tile_pool(name="wstage", bufs=2))
+        loads = ctx.enter_context(tc.tile_pool(name="loads", bufs=3))
+        work = ctx.enter_context(tc.tile_pool(name="work", bufs=3))
+        stores = ctx.enter_context(tc.tile_pool(name="stores", bufs=3))
+        psum_bias = ctx.enter_context(tc.psum_pool(name="psum_bias", bufs=1))
+        psum_tr = ctx.enter_context(tc.psum_pool(name="psum_tr", bufs=2))
+        psum_gate = ctx.enter_context(tc.psum_pool(name="psum_gate", bufs=1))
+
+        xg_v = xg.rearrange("(p s) c -> p s c", s=SLOTS)
+        hx_v = hx.rearrange("(p s) k -> p s k", s=SLOTS)
+        cx_v = cx.rearrange("(p s) k -> p s k", s=SLOTS)
+        out_v = out.rearrange("(p s) c -> p s c", s=SLOTS)
+
+        td_bf = const.tile([P, 2, SLOTS], BF16)
+        nc.scalar.dma_start(out=td_bf[:, 0, :], in_=td0.rearrange("(p s) -> p s", s=SLOTS))
+        nc.scalar.dma_start(out=td_bf[:, 1, :], in_=td1.rearrange("(p s) -> p s", s=SLOTS))
+        a_bf = const.tile([P, 1], BF16)
+        nc.scalar.dma_start(out=a_bf[:], in_=a.partition_broadcast(P))
+        b_bf = const.tile([P, 1], BF16)
+        nc.scalar.dma_start(out=b_bf[:], in_=b.partition_broadcast(P))
+        bias_row = const.tile([P, GATES * OUT], BF16)
+        nc.vector.memset(bias_row[:], 0.0)
+        nc.scalar.dma_start(out=bias_row[0:1, :], in_=b_hh.rearrange("(o n) -> o n", o=1))
+        ones = const.tile([P, P], BF16)
+        nc.vector.memset(ones[:], 1.0)
+        ident = const.tile([P, P], F32)
+        make_identity(nc, ident[:])
+
+        w_hh_v = w_hh.rearrange("(g j p) k -> g p j k", g=GATES, p=P)
+        w_views = [
+            w_hh_v[0],
+            w_pi.rearrange("(j p) k -> p j k", p=P),
+            w_hh_v[1],
+            w_pf.rearrange("(j p) k -> p j k", p=P),
+            w_hh_v[2],
+        ]
+        HH_I, P_I, HH_F, P_F, HH_G = 0, 1, 2, 3, 4
+        w_codes = const.tile([P, len(w_views), OUT], U32, align_bytes=64)
+        w_scales = const.tile([P, len(w_views), OUT], U8, align_bytes=64)
+
+        def transpose_words(dst, rows_bf16):
+            words = rows_bf16.bitcast(F32)
+            for u in range(HALVES):
+                nc.tensor.transpose(dst[:, u, :], words[:, u * P : (u + 1) * P], ident[:])
+
+        for m, w_view in enumerate(w_views):
+            w_raw = wstage.tile([P, W_TILES, K], BF16)
+            nc.sync.dma_start(out=w_raw[:], in_=w_view)
+            w_grouped = wstage.tile([P, OUT, PACK], BF16, align_bytes=64)
+            w_grouped_words = w_grouped[:].bitcast(F32)
+            for half in range(W_TILES // 2):
+                tr = psum_tr.tile([P, 2, HALVES, P], F32, tag="tr")
+                for jj in range(2):
+                    transpose_words(tr[:, jj], w_raw[:, 2 * half + jj, :])
+                cols = slice(2 * half * P, (2 * half + 2) * P)
+                dst = w_grouped_words[:, cols, :].rearrange("p (j n) u -> p j n u", j=2)
+                src = tr[:].rearrange("p j u n -> p j n u")
+                if half == 0:
+                    nc.vector.tensor_copy(out=dst, in_=src)
+                else:
+                    nc.scalar.copy(out=dst, in_=src)
+            nc.vector.quantize_mx(
+                out=w_codes[:, m, :].bitcast(FP8X4),
+                scales=w_scales[:, m, :],
+                in_=w_grouped[:].rearrange("p n t -> p (n t)"),
+            )
+
+        bias_ps = []
+        for g in range(GATES):
+            bias_bank = psum_bias.tile([P, OUT], F32, name="bias_bank%d" % g)
+            nc.tensor.matmul(
+                out=bias_bank[:],
+                lhsT=ones[:],
+                rhs=bias_row[:, g * OUT : (g + 1) * OUT],
+                start=True,
+                stop=True,
+            )
+            bias_ps.append(bias_bank)
+
+        neg_b = const.tile([P, 1], F32)
+        nc.vector.tensor_scalar(
+            out=neg_b[:], in0=b_bf[:], scalar1=-1.0, scalar2=None, op0=ALU.mult
+        )
+        a_f32 = const.tile([P, 1], F32)
+        nc.vector.tensor_copy(out=a_f32[:], in_=a_bf[:])
+        decay_exp = const.tile([P, 2, SLOTS], F32)
+        nc.scalar.activation(out=decay_exp[:], in_=td_bf[:], func=ACT.Exp, scale=neg_b[:, 0:1])
+        decay = const.tile([P, 2, SLOTS], F32)
+        nc.vector.tensor_scalar(
+            out=decay[:], in0=decay_exp[:], scalar1=a_f32[:, 0:1], scalar2=None, op0=ALU.mult
+        )
+
+        HX, CX = 0, 1
+
+        def mx_pass(bank, codes, scales, operand, m, start, stop):
+            nc.tensor.matmul_mx(
+                out=bank[:],
+                lhsT=codes[:, operand, :].bitcast(FP8X4),
+                lhsT_scale=scales[:, operand, :],
+                rhs=w_codes[:, m, :].bitcast(FP8X4),
+                rhs_scale=w_scales[:, m, :],
+                start=start,
+                stop=stop,
+            )
+
+        for chunk in range(N_CHUNKS):
+            slots = slice(chunk * CHUNK, (chunk + 1) * CHUNK)
+            hx_sb = loads.tile([P, CHUNK, K], BF16)
+            nc.sync.dma_start(out=hx_sb[:], in_=hx_v[:, slots, :])
+            cx_sb = loads.tile([P, CHUNK, K], BF16)
+            nc.sync.dma_start(out=cx_sb[:], in_=cx_v[:, slots, :])
+            xg_sb = loads.tile([P, CHUNK, GATES * OUT], BF16)
+            nc.sync.dma_start(out=xg_sb[:], in_=xg_v[:, slots, :])
+            out_sb = stores.tile([P, CHUNK, OUT], F32)
+
+            for i in range(CHUNK):
+                s = chunk * CHUNK + i
+                forcoff = decay[:, 0, s : s + 1]
+                incoff = decay[:, 1, s : s + 1]
+
+                tr = psum_tr.tile([P, 2, HALVES, P], F32, tag="tr")
+                transpose_words(tr[:, HX], hx_sb[:, i, :])
+                transpose_words(tr[:, CX], cx_sb[:, i, :])
+                grouped = work.tile([P, 2, P, PACK], BF16, align_bytes=64)
+                nc.scalar.copy(
+                    out=grouped[:].bitcast(F32), in_=tr[:].rearrange("p o u r -> p o r u")
+                )
+                codes = work.tile([P, 2, P], U32, align_bytes=64)
+                scales = work.tile([P, 2, P], U8, align_bytes=64)
+                nc.vector.quantize_mx(
+                    out=codes[:].rearrange("p o r -> p (o r)").bitcast(FP8X4),
+                    scales=scales[:].rearrange("p o r -> p (o r)"),
+                    in_=grouped[:].rearrange("p o r t -> p (o r t)"),
+                )
+
+                pre = work.tile([P, GATES, OUT], F32)
+                for g in range(GATES):
+                    nc.vector.tensor_tensor(
+                        out=pre[:, g, :],
+                        in0=bias_ps[g][:],
+                        in1=xg_sb[:, i, g * OUT : (g + 1) * OUT],
+                        op=ALU.add,
+                    )
+
+                bank_i = psum_gate.tile([P, OUT], F32)
+                mx_pass(bank_i, codes, scales, HX, HH_I, True, False)
+                mx_pass(bank_i, codes, scales, CX, P_I, False, True)
+                bank_f = psum_gate.tile([P, OUT], F32)
+                mx_pass(bank_f, codes, scales, HX, HH_F, True, False)
+                mx_pass(bank_f, codes, scales, CX, P_F, False, True)
+                bank_g = psum_gate.tile([P, OUT], F32)
+                mx_pass(bank_g, codes, scales, HX, HH_G, True, True)
+
+                for g, bank in enumerate((bank_i, bank_f, bank_g)):
+                    nc.vector.tensor_tensor(
+                        out=pre[:, g, :], in0=bank[:], in1=pre[:, g, :], op=ALU.add
+                    )
+
+                gate = work.tile([P, GATES, OUT], F32)
+                nc.scalar.activation(out=gate[:, 0:2, :], in_=pre[:, 0:2, :], func=ACT.Sigmoid)
+                nc.scalar.activation(out=gate[:, 2, :], in_=pre[:, 2, :], func=ACT.Tanh)
+
+                keep = work.tile([P, OUT], F32)
+                nc.vector.scalar_tensor_tensor(
+                    out=keep[:],
+                    in0=gate[:, 1, :],
+                    scalar=forcoff,
+                    in1=cx_sb[:, i, :],
+                    op0=ALU.mult,
+                    op1=ALU.mult,
+                )
+                fresh = work.tile([P, OUT], F32)
+                nc.vector.scalar_tensor_tensor(
+                    out=fresh[:],
+                    in0=gate[:, 0, :],
+                    scalar=incoff,
+                    in1=gate[:, 2, :],
+                    op0=ALU.mult,
+                    op1=ALU.mult,
+                )
+                nc.vector.tensor_tensor(
+                    out=out_sb[:, i, :], in0=keep[:], in1=fresh[:], op=ALU.add
+                )
+
+            nc.sync.dma_start(out=out_v[:, slots, :], in_=out_sb[:])

@@ -190,30 +190,22 @@ def tile_ircnn_lstmcell_pa_t_kernel(
                         out=pre[:, g, :], in0=bank[:], in1=pre[:, g, :], op=ALU.add
                     )
 
-                gate = work.tile([P, GATES, OUT], F32)
-                nc.scalar.activation(out=gate[:, 0:2, :], in_=pre[:, 0:2, :], func=ACT.Sigmoid)
-                nc.scalar.activation(out=gate[:, 2, :], in_=pre[:, 2, :], func=ACT.Tanh)
+                sig = work.tile([P, 2, OUT], F32)
+                nc.scalar.activation(out=sig[:], in_=pre[:, 0:2, :], func=ACT.Sigmoid)
+                cand = work.tile([P, OUT], F32)
+                nc.scalar.activation(out=cand[:], in_=pre[:, 2, :], func=ACT.Tanh)
+                partner = work.tile([P, 2, OUT], F32)
+                nc.scalar.activation(
+                    out=partner[:, 1, :], in_=cx_sb[:, i, :], func=ACT.Copy, scale=forcoff
+                )
+                nc.scalar.activation(
+                    out=partner[:, 0, :], in_=cand[:], func=ACT.Copy, scale=incoff
+                )
 
-                keep = work.tile([P, OUT], F32)
-                nc.vector.scalar_tensor_tensor(
-                    out=keep[:],
-                    in0=gate[:, 1, :],
-                    scalar=forcoff,
-                    in1=cx_sb[:, i, :],
-                    op0=ALU.mult,
-                    op1=ALU.mult,
-                )
-                fresh = work.tile([P, OUT], F32)
-                nc.vector.scalar_tensor_tensor(
-                    out=fresh[:],
-                    in0=gate[:, 0, :],
-                    scalar=incoff,
-                    in1=gate[:, 2, :],
-                    op0=ALU.mult,
-                    op1=ALU.mult,
-                )
-                nc.vector.tensor_tensor(
-                    out=out_sb[:, i, :], in0=keep[:], in1=fresh[:], op=ALU.add
+                prod = work.tile([P, 2, OUT], F32)
+                nc.gpsimd.tensor_tensor(out=prod[:], in0=sig[:], in1=partner[:], op=ALU.mult)
+                nc.gpsimd.tensor_tensor(
+                    out=out_sb[:, i, :], in0=prod[:, 0, :], in1=prod[:, 1, :], op=ALU.add
                 )
 
             nc.sync.dma_start(out=out_v[:, slots, :], in_=out_sb[:])

@@ -22,6 +22,16 @@ SLOTS = B // P
 CHUNK = 4
 N_CHUNKS = SLOTS // CHUNK
 W_TILES = OUT // P
+HX, CX = 0, 1
+HH_I, P_I, HH_F, P_F, HH_G = 0, 1, 2, 3, 4
+N_WEIGHTS = 5
+
+AHEAD_TRANSPOSE = 3
+AHEAD_PACK = 2
+AHEAD_MATMUL = 1
+AHEAD_BIAS = 4
+BEHIND_COMBINE = 1
+AHEAD_LOAD = 2
 
 FLOPS = 2 * B * K * (GATES * OUT + 2 * OUT)
 
@@ -31,11 +41,20 @@ def tile_ircnn_lstmcell_pa_t_kernel(
 ):
     nc = tc.nc
     with ExitStack() as ctx:
-        const = ctx.enter_context(tc.tile_pool(name="const", bufs=1))
-        wstage = ctx.enter_context(tc.tile_pool(name="wstage", bufs=2))
-        loads = ctx.enter_context(tc.tile_pool(name="loads", bufs=3))
-        work = ctx.enter_context(tc.tile_pool(name="work", bufs=3))
-        stores = ctx.enter_context(tc.tile_pool(name="stores", bufs=3))
+        ctx.enter_context(tc.manual_schedule())
+
+        def pool(name, bufs):
+            return ctx.enter_context(tc.tile_pool(name=name, bufs=bufs))
+
+        const = pool("const", 1)
+        wstage = pool("wstage", 2)
+        loads = pool("loads", AHEAD_LOAD + 1)
+        pre_pool = pool("pre", AHEAD_BIAS + 2)
+        grouped_pool = pool("grouped", 2)
+        packed_pool = pool("packed", AHEAD_PACK + 1)
+        gate_pool = pool("gate", BEHIND_COMBINE + 2)
+        prod_pool = pool("prod", 2)
+        store_pool = pool("store", 4)
         psum_bias = ctx.enter_context(tc.psum_pool(name="psum_bias", bufs=1))
         psum_tr = ctx.enter_context(tc.psum_pool(name="psum_tr", bufs=2))
         psum_gate = ctx.enter_context(tc.psum_pool(name="psum_gate", bufs=1))
@@ -45,6 +64,115 @@ def tile_ircnn_lstmcell_pa_t_kernel(
         cx_v = cx.rearrange("(p s) k -> p s k", s=SLOTS)
         out_v = out.rearrange("(p s) c -> p s c", s=SLOTS)
 
+        hx_sb, cx_sb, xg_sb = {}, {}, {}
+        tr_ps, codes_sb, scales_sb, pre_sb, banks_ps, sig_sb, partner_sb = {}, {}, {}, {}, {}, {}, {}
+
+        def load_chunk(c):
+            slots = slice(c * CHUNK, (c + 1) * CHUNK)
+            xg_sb[c] = loads.tile([P, CHUNK, GATES * OUT], BF16, name="xg_sb")
+            nc.sync.dma_start(out=xg_sb[c][:], in_=xg_v[:, slots, :])
+            hx_sb[c] = loads.tile([P, CHUNK, K], BF16, name="hx_sb")
+            nc.sync.dma_start(out=hx_sb[c][:], in_=hx_v[:, slots, :])
+            cx_sb[c] = loads.tile([P, CHUNK, K], BF16, name="cx_sb")
+            nc.sync.dma_start(out=cx_sb[c][:], in_=cx_v[:, slots, :])
+
+        def transpose_words(dst, rows_bf16):
+            words = rows_bf16.bitcast(F32)
+            for u in range(HALVES):
+                nc.tensor.transpose(dst[:, u, :], words[:, u * P : (u + 1) * P], ident[:])
+
+        def stage_bias(s):
+            c, i = divmod(s, CHUNK)
+            pre_sb[s] = pre_pool.tile([P, GATES, OUT], F32, name="pre")
+            for g in range(GATES):
+                nc.vector.tensor_tensor(
+                    out=pre_sb[s][:, g, :],
+                    in0=bias_ps[g][:],
+                    in1=xg_sb[c][:, i, g * OUT : (g + 1) * OUT],
+                    op=ALU.add,
+                )
+
+        def stage_transpose(s):
+            c, i = divmod(s, CHUNK)
+            tr_ps[s] = psum_tr.tile([P, 2, HALVES, P], F32, name="tr")
+            transpose_words(tr_ps[s][:, HX], hx_sb[c][:, i, :])
+            transpose_words(tr_ps[s][:, CX], cx_sb[c][:, i, :])
+
+        def stage_pack(s):
+            grouped = grouped_pool.tile([P, 2, P, PACK], BF16, align_bytes=64)
+            nc.scalar.copy(
+                out=grouped[:].bitcast(F32), in_=tr_ps[s][:].rearrange("p o u r -> p o r u")
+            )
+            codes_sb[s] = packed_pool.tile([P, 2, P], U32, align_bytes=64, name="codes")
+            scales_sb[s] = packed_pool.tile([P, 2, P], U8, align_bytes=64, name="scales")
+            nc.vector.quantize_mx(
+                out=codes_sb[s][:].rearrange("p o r -> p (o r)").bitcast(FP8X4),
+                scales=scales_sb[s][:].rearrange("p o r -> p (o r)"),
+                in_=grouped[:].rearrange("p o r t -> p (o r t)"),
+            )
+
+        def mx_pass(bank, s, operand, m, start, stop):
+            nc.tensor.matmul_mx(
+                out=bank[:],
+                lhsT=codes_sb[s][:, operand, :].bitcast(FP8X4),
+                lhsT_scale=scales_sb[s][:, operand, :],
+                rhs=w_codes[:, m, :].bitcast(FP8X4),
+                rhs_scale=w_scales[:, m, :],
+                start=start,
+                stop=stop,
+            )
+
+        def stage_matmul(s):
+            bank_i = psum_gate.tile([P, OUT], F32)
+            mx_pass(bank_i, s, HX, HH_I, True, False)
+            mx_pass(bank_i, s, CX, P_I, False, True)
+            bank_f = psum_gate.tile([P, OUT], F32)
+            mx_pass(bank_f, s, HX, HH_F, True, False)
+            mx_pass(bank_f, s, CX, P_F, False, True)
+            bank_g = psum_gate.tile([P, OUT], F32)
+            mx_pass(bank_g, s, HX, HH_G, True, True)
+            banks_ps[s] = (bank_i, bank_f, bank_g)
+
+        def stage_sum(s):
+            for g in range(GATES):
+                nc.vector.tensor_tensor(
+                    out=pre_sb[s][:, g, :],
+                    in0=banks_ps[s][g][:],
+                    in1=pre_sb[s][:, g, :],
+                    op=ALU.add,
+                )
+
+        def stage_gates(s):
+            c, i = divmod(s, CHUNK)
+            sig_sb[s] = gate_pool.tile([P, 2, OUT], F32, name="sig")
+            nc.scalar.activation(out=sig_sb[s][:], in_=pre_sb[s][:, 0:2, :], func=ACT.Sigmoid)
+            cand = gate_pool.tile([P, OUT], F32)
+            nc.scalar.activation(out=cand[:], in_=pre_sb[s][:, 2, :], func=ACT.Tanh)
+            partner_sb[s] = gate_pool.tile([P, 2, OUT], F32, name="partner")
+            nc.scalar.activation(
+                out=partner_sb[s][:, 1, :],
+                in_=cx_sb[c][:, i, :],
+                func=ACT.Copy,
+                scale=decay[:, 0, s : s + 1],
+            )
+            nc.scalar.activation(
+                out=partner_sb[s][:, 0, :], in_=cand[:], func=ACT.Copy, scale=decay[:, 1, s : s + 1]
+            )
+
+        def stage_combine(s):
+            prod = prod_pool.tile([P, 2, OUT], F32)
+            nc.gpsimd.tensor_tensor(
+                out=prod[:], in0=sig_sb[s][:], in1=partner_sb[s][:], op=ALU.mult
+            )
+            out_sb = store_pool.tile([P, OUT], F32)
+            nc.gpsimd.tensor_tensor(
+                out=out_sb[:], in0=prod[:, 0, :], in1=prod[:, 1, :], op=ALU.add
+            )
+            nc.sync.dma_start(out=out_v[:, s, :], in_=out_sb[:])
+
+        bias_row = const.tile([P, GATES * OUT], BF16)
+        nc.vector.memset(bias_row[:], 0.0)
+        nc.scalar.dma_start(out=bias_row[0:1, :], in_=b_hh.rearrange("(o n) -> o n", o=1))
         td_bf = const.tile([P, 2, SLOTS], BF16)
         nc.scalar.dma_start(out=td_bf[:, 0, :], in_=td0.rearrange("(p s) -> p s", s=SLOTS))
         nc.scalar.dma_start(out=td_bf[:, 1, :], in_=td1.rearrange("(p s) -> p s", s=SLOTS))
@@ -52,52 +180,27 @@ def tile_ircnn_lstmcell_pa_t_kernel(
         nc.scalar.dma_start(out=a_bf[:], in_=a.partition_broadcast(P))
         b_bf = const.tile([P, 1], BF16)
         nc.scalar.dma_start(out=b_bf[:], in_=b.partition_broadcast(P))
-        bias_row = const.tile([P, GATES * OUT], BF16)
-        nc.vector.memset(bias_row[:], 0.0)
-        nc.scalar.dma_start(out=bias_row[0:1, :], in_=b_hh.rearrange("(o n) -> o n", o=1))
         ones = const.tile([P, P], BF16)
         nc.vector.memset(ones[:], 1.0)
         ident = const.tile([P, P], F32)
         make_identity(nc, ident[:])
 
+        load_chunk(0)
+
         w_hh_v = w_hh.rearrange("(g j p) k -> g p j k", g=GATES, p=P)
-        w_views = [
-            w_hh_v[0],
-            w_pi.rearrange("(j p) k -> p j k", p=P),
-            w_hh_v[1],
-            w_pf.rearrange("(j p) k -> p j k", p=P),
-            w_hh_v[2],
-        ]
-        HH_I, P_I, HH_F, P_F, HH_G = 0, 1, 2, 3, 4
-        w_codes = const.tile([P, len(w_views), OUT], U32, align_bytes=64)
-        w_scales = const.tile([P, len(w_views), OUT], U8, align_bytes=64)
-
-        def transpose_words(dst, rows_bf16):
-            words = rows_bf16.bitcast(F32)
-            for u in range(HALVES):
-                nc.tensor.transpose(dst[:, u, :], words[:, u * P : (u + 1) * P], ident[:])
-
-        for m, w_view in enumerate(w_views):
-            w_raw = wstage.tile([P, W_TILES, K], BF16)
-            nc.sync.dma_start(out=w_raw[:], in_=w_view)
-            w_grouped = wstage.tile([P, OUT, PACK], BF16, align_bytes=64)
-            w_grouped_words = w_grouped[:].bitcast(F32)
-            for half in range(W_TILES // 2):
-                tr = psum_tr.tile([P, 2, HALVES, P], F32, tag="tr")
-                for jj in range(2):
-                    transpose_words(tr[:, jj], w_raw[:, 2 * half + jj, :])
-                cols = slice(2 * half * P, (2 * half + 2) * P)
-                dst = w_grouped_words[:, cols, :].rearrange("p (j n) u -> p j n u", j=2)
-                src = tr[:].rearrange("p j u n -> p j n u")
-                if half == 0:
-                    nc.vector.tensor_copy(out=dst, in_=src)
-                else:
-                    nc.scalar.copy(out=dst, in_=src)
-            nc.vector.quantize_mx(
-                out=w_codes[:, m, :].bitcast(FP8X4),
-                scales=w_scales[:, m, :],
-                in_=w_grouped[:].rearrange("p n t -> p (n t)"),
-            )
+        w_views = {
+            HH_I: w_hh_v[0],
+            P_I: w_pi.rearrange("(j p) k -> p j k", p=P),
+            HH_F: w_hh_v[1],
+            P_F: w_pf.rearrange("(j p) k -> p j k", p=P),
+            HH_G: w_hh_v[2],
+        }
+        w_raw = {}
+        for m in range(N_WEIGHTS):
+            w_raw[m] = const.tile([P, W_TILES, K], BF16, name="w_raw%d" % m)
+            nc.sync.dma_start(out=w_raw[m][:], in_=w_views[m])
+        for c in range(1, AHEAD_LOAD):
+            load_chunk(c)
 
         bias_ps = []
         for g in range(GATES):
@@ -110,6 +213,28 @@ def tile_ircnn_lstmcell_pa_t_kernel(
                 stop=True,
             )
             bias_ps.append(bias_bank)
+
+        w_codes = const.tile([P, N_WEIGHTS, OUT], U32, align_bytes=64)
+        w_scales = const.tile([P, N_WEIGHTS, OUT], U8, align_bytes=64)
+        for m in range(N_WEIGHTS):
+            if m < AHEAD_BIAS:
+                stage_bias(m)
+            w_grouped = wstage.tile([P, OUT, PACK], BF16, align_bytes=64)
+            w_grouped_words = w_grouped[:].bitcast(F32)
+            for pair in range(W_TILES // 2):
+                tr = psum_tr.tile([P, 2, HALVES, P], F32, name="tr")
+                for jj in range(2):
+                    transpose_words(tr[:, jj], w_raw[m][:, 2 * pair + jj, :])
+                cols = slice(2 * pair * P, (2 * pair + 2) * P)
+                nc.scalar.copy(
+                    out=w_grouped_words[:, cols, :].rearrange("p (j n) u -> p j n u", j=2),
+                    in_=tr[:].rearrange("p j u n -> p j n u"),
+                )
+            nc.vector.quantize_mx(
+                out=w_codes[:, m, :].bitcast(FP8X4),
+                scales=w_scales[:, m, :],
+                in_=w_grouped[:].rearrange("p n t -> p (n t)"),
+            )
 
         neg_b = const.tile([P, 1], F32)
         nc.vector.tensor_scalar(
@@ -124,88 +249,23 @@ def tile_ircnn_lstmcell_pa_t_kernel(
             out=decay[:], in0=decay_exp[:], scalar1=a_f32[:, 0:1], scalar2=None, op0=ALU.mult
         )
 
-        HX, CX = 0, 1
+        def in_range(s):
+            return 0 <= s < SLOTS
 
-        def mx_pass(bank, codes, scales, operand, m, start, stop):
-            nc.tensor.matmul_mx(
-                out=bank[:],
-                lhsT=codes[:, operand, :].bitcast(FP8X4),
-                lhsT_scale=scales[:, operand, :],
-                rhs=w_codes[:, m, :].bitcast(FP8X4),
-                rhs_scale=w_scales[:, m, :],
-                start=start,
-                stop=stop,
-            )
-
-        for chunk in range(N_CHUNKS):
-            slots = slice(chunk * CHUNK, (chunk + 1) * CHUNK)
-            hx_sb = loads.tile([P, CHUNK, K], BF16)
-            nc.sync.dma_start(out=hx_sb[:], in_=hx_v[:, slots, :])
-            cx_sb = loads.tile([P, CHUNK, K], BF16)
-            nc.sync.dma_start(out=cx_sb[:], in_=cx_v[:, slots, :])
-            xg_sb = loads.tile([P, CHUNK, GATES * OUT], BF16)
-            nc.sync.dma_start(out=xg_sb[:], in_=xg_v[:, slots, :])
-            out_sb = stores.tile([P, CHUNK, OUT], F32)
-
-            for i in range(CHUNK):
-                s = chunk * CHUNK + i
-                forcoff = decay[:, 0, s : s + 1]
-                incoff = decay[:, 1, s : s + 1]
-
-                tr = psum_tr.tile([P, 2, HALVES, P], F32, tag="tr")
-                transpose_words(tr[:, HX], hx_sb[:, i, :])
-                transpose_words(tr[:, CX], cx_sb[:, i, :])
-                grouped = work.tile([P, 2, P, PACK], BF16, align_bytes=64)
-                nc.scalar.copy(
-                    out=grouped[:].bitcast(F32), in_=tr[:].rearrange("p o u r -> p o r u")
-                )
-                codes = work.tile([P, 2, P], U32, align_bytes=64)
-                scales = work.tile([P, 2, P], U8, align_bytes=64)
-                nc.vector.quantize_mx(
-                    out=codes[:].rearrange("p o r -> p (o r)").bitcast(FP8X4),
-                    scales=scales[:].rearrange("p o r -> p (o r)"),
-                    in_=grouped[:].rearrange("p o r t -> p (o r t)"),
-                )
-
-                pre = work.tile([P, GATES, OUT], F32)
-                for g in range(GATES):
-                    nc.vector.tensor_tensor(
-                        out=pre[:, g, :],
-                        in0=bias_ps[g][:],
-                        in1=xg_sb[:, i, g * OUT : (g + 1) * OUT],
-                        op=ALU.add,
-                    )
-
-                bank_i = psum_gate.tile([P, OUT], F32)
-                mx_pass(bank_i, codes, scales, HX, HH_I, True, False)
-                mx_pass(bank_i, codes, scales, CX, P_I, False, True)
-                bank_f = psum_gate.tile([P, OUT], F32)
-                mx_pass(bank_f, codes, scales, HX, HH_F, True, False)
-                mx_pass(bank_f, codes, scales, CX, P_F, False, True)
-                bank_g = psum_gate.tile([P, OUT], F32)
-                mx_pass(bank_g, codes, scales, HX, HH_G, True, True)
-
-                for g, bank in enumerate((bank_i, bank_f, bank_g)):
-                    nc.vector.tensor_tensor(
-                        out=pre[:, g, :], in0=bank[:], in1=pre[:, g, :], op=ALU.add
-                    )
-
-                sig = work.tile([P, 2, OUT], F32)
-                nc.scalar.activation(out=sig[:], in_=pre[:, 0:2, :], func=ACT.Sigmoid)
-                cand = work.tile([P, OUT], F32)
-                nc.scalar.activation(out=cand[:], in_=pre[:, 2, :], func=ACT.Tanh)
-                partner = work.tile([P, 2, OUT], F32)
-                nc.scalar.activation(
-                    out=partner[:, 1, :], in_=cx_sb[:, i, :], func=ACT.Copy, scale=forcoff
-                )
-                nc.scalar.activation(
-                    out=partner[:, 0, :], in_=cand[:], func=ACT.Copy, scale=incoff
-                )
-
-                prod = work.tile([P, 2, OUT], F32)
-                nc.gpsimd.tensor_tensor(out=prod[:], in0=sig[:], in1=partner[:], op=ALU.mult)
-                nc.gpsimd.tensor_tensor(
-                    out=out_sb[:, i, :], in0=prod[:, 0, :], in1=prod[:, 1, :], op=ALU.add
-                )
-
-            nc.sync.dma_start(out=out_v[:, slots, :], in_=out_sb[:])
+        for step in range(-AHEAD_TRANSPOSE, SLOTS + BEHIND_COMBINE):
+            if step >= 0 and step % CHUNK == 0 and step // CHUNK + AHEAD_LOAD < N_CHUNKS:
+                load_chunk(step // CHUNK + AHEAD_LOAD)
+            if in_range(step):
+                stage_sum(step)
+            if in_range(step + AHEAD_PACK):
+                stage_pack(step + AHEAD_PACK)
+            if in_range(step + AHEAD_MATMUL):
+                stage_matmul(step + AHEAD_MATMUL)
+            if in_range(step + AHEAD_TRANSPOSE):
+                stage_transpose(step + AHEAD_TRANSPOSE)
+            if step >= 0 and in_range(step + AHEAD_BIAS):
+                stage_bias(step + AHEAD_BIAS)
+            if in_range(step):
+                stage_gates(step)
+            if in_range(step - BEHIND_COMBINE):
+                stage_combine(step - BEHIND_COMBINE)

@@ -19,7 +19,7 @@ GATES = 3
 PACK = 4
 HALVES = 2
 SLOTS = B // P
-CHUNK = 4
+CHUNK = 2
 N_CHUNKS = SLOTS // CHUNK
 W_TILES = OUT // P
 HX, CX = 0, 1
@@ -31,7 +31,7 @@ AHEAD_PACK = 2
 AHEAD_MATMUL = 1
 AHEAD_BIAS = 4
 BEHIND_COMBINE = 1
-AHEAD_LOAD = 2
+AHEAD_LOAD = 3
 
 FLOPS = 2 * B * K * (GATES * OUT + 2 * OUT)
 
@@ -48,13 +48,14 @@ def tile_ircnn_lstmcell_pa_t_kernel(
 
         const = pool("const", 1)
         wstage = pool("wstage", 2)
-        loads = pool("loads", AHEAD_LOAD + 1)
+        loads = pool("loads", AHEAD_LOAD + 2)
         pre_pool = pool("pre", AHEAD_BIAS + 2)
         grouped_pool = pool("grouped", 2)
         packed_pool = pool("packed", AHEAD_PACK + 1)
-        gate_pool = pool("gate", BEHIND_COMBINE + 2)
+        cand_pool = pool("cand", 2)
+        gate_pool = pool("gate", 3)
         prod_pool = pool("prod", 2)
-        store_pool = pool("store", 4)
+        store_pool = pool("store", 3)
         psum_bias = ctx.enter_context(tc.psum_pool(name="psum_bias", bufs=1))
         psum_tr = ctx.enter_context(tc.psum_pool(name="psum_tr", bufs=2))
         psum_gate = ctx.enter_context(tc.psum_pool(name="psum_gate", bufs=1))
@@ -144,31 +145,37 @@ def tile_ircnn_lstmcell_pa_t_kernel(
 
         def stage_gates(s):
             c, i = divmod(s, CHUNK)
-            sig_sb[s] = gate_pool.tile([P, 2, OUT], F32, name="sig")
-            nc.scalar.activation(out=sig_sb[s][:], in_=pre_sb[s][:, 0:2, :], func=ACT.Sigmoid)
-            cand = gate_pool.tile([P, OUT], F32)
-            nc.scalar.activation(out=cand[:], in_=pre_sb[s][:, 2, :], func=ACT.Tanh)
-            partner_sb[s] = gate_pool.tile([P, 2, OUT], F32, name="partner")
+            if i == 0:
+                sig_sb[c] = gate_pool.tile([P, CHUNK, 2, OUT], F32, name="sig")
+                partner_sb[c] = gate_pool.tile([P, CHUNK, 2, OUT], F32, name="partner")
             nc.scalar.activation(
-                out=partner_sb[s][:, 1, :],
+                out=sig_sb[c][:, i, :, :], in_=pre_sb[s][:, 0:2, :], func=ACT.Sigmoid
+            )
+            cand = cand_pool.tile([P, OUT], F32)
+            nc.scalar.activation(out=cand[:], in_=pre_sb[s][:, 2, :], func=ACT.Tanh)
+            nc.scalar.activation(
+                out=partner_sb[c][:, i, 1, :],
                 in_=cx_sb[c][:, i, :],
                 func=ACT.Copy,
                 scale=decay[:, 0, s : s + 1],
             )
             nc.scalar.activation(
-                out=partner_sb[s][:, 0, :], in_=cand[:], func=ACT.Copy, scale=decay[:, 1, s : s + 1]
+                out=partner_sb[c][:, i, 0, :],
+                in_=cand[:],
+                func=ACT.Copy,
+                scale=decay[:, 1, s : s + 1],
             )
 
-        def stage_combine(s):
-            prod = prod_pool.tile([P, 2, OUT], F32)
+        def stage_combine(c):
+            prod = prod_pool.tile([P, CHUNK, 2, OUT], F32)
             nc.gpsimd.tensor_tensor(
-                out=prod[:], in0=sig_sb[s][:], in1=partner_sb[s][:], op=ALU.mult
+                out=prod[:], in0=sig_sb[c][:], in1=partner_sb[c][:], op=ALU.mult
             )
-            out_sb = store_pool.tile([P, OUT], F32)
+            out_sb = store_pool.tile([P, CHUNK, OUT], F32)
             nc.gpsimd.tensor_tensor(
-                out=out_sb[:], in0=prod[:, 0, :], in1=prod[:, 1, :], op=ALU.add
+                out=out_sb[:], in0=prod[:, :, 0, :], in1=prod[:, :, 1, :], op=ALU.add
             )
-            nc.sync.dma_start(out=out_v[:, s, :], in_=out_sb[:])
+            nc.sync.dma_start(out=out_v[:, c * CHUNK : (c + 1) * CHUNK, :], in_=out_sb[:])
 
         bias_row = const.tile([P, GATES * OUT], BF16)
         nc.vector.memset(bias_row[:], 0.0)
@@ -185,7 +192,8 @@ def tile_ircnn_lstmcell_pa_t_kernel(
         ident = const.tile([P, P], F32)
         make_identity(nc, ident[:])
 
-        load_chunk(0)
+        for c in range(AHEAD_BIAS // CHUNK):
+            load_chunk(c)
 
         w_hh_v = w_hh.rearrange("(g j p) k -> g p j k", g=GATES, p=P)
         w_views = {
@@ -199,7 +207,7 @@ def tile_ircnn_lstmcell_pa_t_kernel(
         for m in range(N_WEIGHTS):
             w_raw[m] = const.tile([P, W_TILES, K], BF16, name="w_raw%d" % m)
             nc.sync.dma_start(out=w_raw[m][:], in_=w_views[m])
-        for c in range(1, AHEAD_LOAD):
+        for c in range(AHEAD_BIAS // CHUNK, AHEAD_LOAD):
             load_chunk(c)
 
         bias_ps = []
@@ -267,5 +275,5 @@ def tile_ircnn_lstmcell_pa_t_kernel(
                 stage_bias(step + AHEAD_BIAS)
             if in_range(step):
                 stage_gates(step)
-            if in_range(step - BEHIND_COMBINE):
-                stage_combine(step - BEHIND_COMBINE)
+            if step >= CHUNK and step % CHUNK == 0:
+                stage_combine(step // CHUNK - 1)

@@ -19,19 +19,20 @@ GATES = 3
 PACK = 4
 HALVES = 2
 SLOTS = B // P
-CHUNK = 2
+CHUNK = 4
 N_CHUNKS = SLOTS // CHUNK
 W_TILES = OUT // P
 HX, CX = 0, 1
 HH_I, P_I, HH_F, P_F, HH_G = 0, 1, 2, 3, 4
 N_WEIGHTS = 5
 
-AHEAD_TRANSPOSE = 3
-AHEAD_PACK = 2
+AHEAD_TRANSPOSE = 7
+AHEAD_COPY = 6
 AHEAD_MATMUL = 1
 AHEAD_BIAS = 4
 BEHIND_COMBINE = 1
-AHEAD_LOAD = 3
+AHEAD_LOAD_XG = 2
+AHEAD_LOAD_STATE = 3
 
 FLOPS = 2 * B * K * (GATES * OUT + 2 * OUT)
 
@@ -48,14 +49,15 @@ def tile_ircnn_lstmcell_pa_t_kernel(
 
         const = pool("const", 1)
         wstage = pool("wstage", 2)
-        loads = pool("loads", AHEAD_LOAD + 2)
+        xg_pool = pool("xg", AHEAD_LOAD_XG + 1)
+        hx_pool = pool("hx", AHEAD_LOAD_STATE)
+        cx_pool = pool("cx", AHEAD_LOAD_STATE + 2)
         pre_pool = pool("pre", AHEAD_BIAS + 2)
         grouped_pool = pool("grouped", 2)
-        packed_pool = pool("packed", AHEAD_PACK + 1)
-        cand_pool = pool("cand", 2)
-        gate_pool = pool("gate", 3)
+        packed_pool = pool("packed", 2)
+        gate_pool = pool("gate", BEHIND_COMBINE + 2)
         prod_pool = pool("prod", 2)
-        store_pool = pool("store", 3)
+        store_pool = pool("store", 4)
         psum_bias = ctx.enter_context(tc.psum_pool(name="psum_bias", bufs=1))
         psum_tr = ctx.enter_context(tc.psum_pool(name="psum_tr", bufs=2))
         psum_gate = ctx.enter_context(tc.psum_pool(name="psum_gate", bufs=1))
@@ -66,16 +68,18 @@ def tile_ircnn_lstmcell_pa_t_kernel(
         out_v = out.rearrange("(p s) c -> p s c", s=SLOTS)
 
         hx_sb, cx_sb, xg_sb = {}, {}, {}
-        tr_ps, codes_sb, scales_sb, pre_sb, banks_ps, sig_sb, partner_sb = {}, {}, {}, {}, {}, {}, {}
+        grouped_sb, codes_sb, scales_sb = {}, {}, {}
+        tr_ps, pre_sb, banks_ps, sig_sb, partner_sb = {}, {}, {}, {}, {}
 
-        def load_chunk(c):
-            slots = slice(c * CHUNK, (c + 1) * CHUNK)
-            xg_sb[c] = loads.tile([P, CHUNK, GATES * OUT], BF16, name="xg_sb")
-            nc.sync.dma_start(out=xg_sb[c][:], in_=xg_v[:, slots, :])
-            hx_sb[c] = loads.tile([P, CHUNK, K], BF16, name="hx_sb")
-            nc.sync.dma_start(out=hx_sb[c][:], in_=hx_v[:, slots, :])
-            cx_sb[c] = loads.tile([P, CHUNK, K], BF16, name="cx_sb")
-            nc.sync.dma_start(out=cx_sb[c][:], in_=cx_v[:, slots, :])
+        def load_xg(c):
+            xg_sb[c] = xg_pool.tile([P, CHUNK, GATES * OUT], BF16, name="xg_sb")
+            nc.sync.dma_start(out=xg_sb[c][:], in_=xg_v[:, c * CHUNK : (c + 1) * CHUNK, :])
+
+        def load_state(c):
+            hx_sb[c] = hx_pool.tile([P, CHUNK, K], BF16, name="hx_sb")
+            nc.sync.dma_start(out=hx_sb[c][:], in_=hx_v[:, c * CHUNK : (c + 1) * CHUNK, :])
+            cx_sb[c] = cx_pool.tile([P, CHUNK, K], BF16, name="cx_sb")
+            nc.sync.dma_start(out=cx_sb[c][:], in_=cx_v[:, c * CHUNK : (c + 1) * CHUNK, :])
 
         def transpose_words(dst, rows_bf16):
             words = rows_bf16.bitcast(F32)
@@ -99,24 +103,31 @@ def tile_ircnn_lstmcell_pa_t_kernel(
             transpose_words(tr_ps[s][:, HX], hx_sb[c][:, i, :])
             transpose_words(tr_ps[s][:, CX], cx_sb[c][:, i, :])
 
-        def stage_pack(s):
-            grouped = grouped_pool.tile([P, 2, P, PACK], BF16, align_bytes=64)
+        def stage_copy(s):
+            c, i = divmod(s, CHUNK)
+            if i == 0:
+                grouped_sb[c] = grouped_pool.tile(
+                    [P, CHUNK, 2, P, PACK], BF16, align_bytes=64, name="grouped"
+                )
             nc.scalar.copy(
-                out=grouped[:].bitcast(F32), in_=tr_ps[s][:].rearrange("p o u r -> p o r u")
+                out=grouped_sb[c][:, i].bitcast(F32),
+                in_=tr_ps[s][:].rearrange("p o u r -> p o r u"),
             )
-            codes_sb[s] = packed_pool.tile([P, 2, P], U32, align_bytes=64, name="codes")
-            scales_sb[s] = packed_pool.tile([P, 2, P], U8, align_bytes=64, name="scales")
-            nc.vector.quantize_mx(
-                out=codes_sb[s][:].rearrange("p o r -> p (o r)").bitcast(FP8X4),
-                scales=scales_sb[s][:].rearrange("p o r -> p (o r)"),
-                in_=grouped[:].rearrange("p o r t -> p (o r t)"),
-            )
+            if i == CHUNK - 1:
+                codes_sb[c] = packed_pool.tile([P, CHUNK, 2, P], U32, align_bytes=64, name="codes")
+                scales_sb[c] = packed_pool.tile([P, CHUNK, 2, P], U8, align_bytes=64, name="scales")
+                nc.vector.quantize_mx(
+                    out=codes_sb[c][:].rearrange("p i o r -> p (i o r)").bitcast(FP8X4),
+                    scales=scales_sb[c][:].rearrange("p i o r -> p (i o r)"),
+                    in_=grouped_sb[c][:].rearrange("p i o r t -> p (i o r t)"),
+                )
 
         def mx_pass(bank, s, operand, m, start, stop):
+            c, i = divmod(s, CHUNK)
             nc.tensor.matmul_mx(
                 out=bank[:],
-                lhsT=codes_sb[s][:, operand, :].bitcast(FP8X4),
-                lhsT_scale=scales_sb[s][:, operand, :],
+                lhsT=codes_sb[c][:, i, operand, :].bitcast(FP8X4),
+                lhsT_scale=scales_sb[c][:, i, operand, :],
                 rhs=w_codes[:, m, :].bitcast(FP8X4),
                 rhs_scale=w_scales[:, m, :],
                 start=start,
@@ -145,37 +156,31 @@ def tile_ircnn_lstmcell_pa_t_kernel(
 
         def stage_gates(s):
             c, i = divmod(s, CHUNK)
-            if i == 0:
-                sig_sb[c] = gate_pool.tile([P, CHUNK, 2, OUT], F32, name="sig")
-                partner_sb[c] = gate_pool.tile([P, CHUNK, 2, OUT], F32, name="partner")
-            nc.scalar.activation(
-                out=sig_sb[c][:, i, :, :], in_=pre_sb[s][:, 0:2, :], func=ACT.Sigmoid
-            )
-            cand = cand_pool.tile([P, OUT], F32)
+            sig_sb[s] = gate_pool.tile([P, 2, OUT], F32, name="sig")
+            nc.scalar.activation(out=sig_sb[s][:], in_=pre_sb[s][:, 0:2, :], func=ACT.Sigmoid)
+            cand = gate_pool.tile([P, OUT], F32)
             nc.scalar.activation(out=cand[:], in_=pre_sb[s][:, 2, :], func=ACT.Tanh)
+            partner_sb[s] = gate_pool.tile([P, 2, OUT], F32, name="partner")
             nc.scalar.activation(
-                out=partner_sb[c][:, i, 1, :],
+                out=partner_sb[s][:, 1, :],
                 in_=cx_sb[c][:, i, :],
                 func=ACT.Copy,
                 scale=decay[:, 0, s : s + 1],
             )
             nc.scalar.activation(
-                out=partner_sb[c][:, i, 0, :],
-                in_=cand[:],
-                func=ACT.Copy,
-                scale=decay[:, 1, s : s + 1],
+                out=partner_sb[s][:, 0, :], in_=cand[:], func=ACT.Copy, scale=decay[:, 1, s : s + 1]
             )
 
-        def stage_combine(c):
-            prod = prod_pool.tile([P, CHUNK, 2, OUT], F32)
+        def stage_combine(s):
+            prod = prod_pool.tile([P, 2, OUT], F32)
             nc.gpsimd.tensor_tensor(
-                out=prod[:], in0=sig_sb[c][:], in1=partner_sb[c][:], op=ALU.mult
+                out=prod[:], in0=sig_sb[s][:], in1=partner_sb[s][:], op=ALU.mult
             )
-            out_sb = store_pool.tile([P, CHUNK, OUT], F32)
+            out_sb = store_pool.tile([P, OUT], F32)
             nc.gpsimd.tensor_tensor(
-                out=out_sb[:], in0=prod[:, :, 0, :], in1=prod[:, :, 1, :], op=ALU.add
+                out=out_sb[:], in0=prod[:, 0, :], in1=prod[:, 1, :], op=ALU.add
             )
-            nc.sync.dma_start(out=out_v[:, c * CHUNK : (c + 1) * CHUNK, :], in_=out_sb[:])
+            nc.sync.dma_start(out=out_v[:, s, :], in_=out_sb[:])
 
         bias_row = const.tile([P, GATES * OUT], BF16)
         nc.vector.memset(bias_row[:], 0.0)
@@ -192,8 +197,8 @@ def tile_ircnn_lstmcell_pa_t_kernel(
         ident = const.tile([P, P], F32)
         make_identity(nc, ident[:])
 
-        for c in range(AHEAD_BIAS // CHUNK):
-            load_chunk(c)
+        load_xg(0)
+        load_state(0)
 
         w_hh_v = w_hh.rearrange("(g j p) k -> g p j k", g=GATES, p=P)
         w_views = {
@@ -207,8 +212,10 @@ def tile_ircnn_lstmcell_pa_t_kernel(
         for m in range(N_WEIGHTS):
             w_raw[m] = const.tile([P, W_TILES, K], BF16, name="w_raw%d" % m)
             nc.sync.dma_start(out=w_raw[m][:], in_=w_views[m])
-        for c in range(AHEAD_BIAS // CHUNK, AHEAD_LOAD):
-            load_chunk(c)
+        for c in range(1, AHEAD_LOAD_STATE):
+            load_state(c)
+            if c < AHEAD_LOAD_XG:
+                load_xg(c)
 
         bias_ps = []
         for g in range(GATES):
@@ -261,12 +268,15 @@ def tile_ircnn_lstmcell_pa_t_kernel(
             return 0 <= s < SLOTS
 
         for step in range(-AHEAD_TRANSPOSE, SLOTS + BEHIND_COMBINE):
-            if step >= 0 and step % CHUNK == 0 and step // CHUNK + AHEAD_LOAD < N_CHUNKS:
-                load_chunk(step // CHUNK + AHEAD_LOAD)
+            if step >= 0 and step % CHUNK == 0:
+                if step // CHUNK + AHEAD_LOAD_STATE < N_CHUNKS:
+                    load_state(step // CHUNK + AHEAD_LOAD_STATE)
+                if step // CHUNK + AHEAD_LOAD_XG < N_CHUNKS:
+                    load_xg(step // CHUNK + AHEAD_LOAD_XG)
             if in_range(step):
                 stage_sum(step)
-            if in_range(step + AHEAD_PACK):
-                stage_pack(step + AHEAD_PACK)
+            if in_range(step + AHEAD_COPY):
+                stage_copy(step + AHEAD_COPY)
             if in_range(step + AHEAD_MATMUL):
                 stage_matmul(step + AHEAD_MATMUL)
             if in_range(step + AHEAD_TRANSPOSE):
@@ -275,5 +285,5 @@ def tile_ircnn_lstmcell_pa_t_kernel(
                 stage_bias(step + AHEAD_BIAS)
             if in_range(step):
                 stage_gates(step)
-            if step >= CHUNK and step % CHUNK == 0:
-                stage_combine(step // CHUNK - 1)
+            if in_range(step - BEHIND_COMBINE):
+                stage_combine(step - BEHIND_COMBINE)

@@ -29,10 +29,12 @@ N_WEIGHTS = 5
 AHEAD_TRANSPOSE = 7
 AHEAD_COPY = 6
 AHEAD_MATMUL = 1
-AHEAD_BIAS = 4
+AHEAD_BIAS = 1
 BEHIND_COMBINE = 1
-AHEAD_LOAD_XG = 2
+AHEAD_LOAD_XG = 6
 AHEAD_LOAD_STATE = 3
+
+VECTOR_EVERY = 16
 
 FLOPS = 2 * B * K * (GATES * OUT + 2 * OUT)
 
@@ -49,7 +51,7 @@ def tile_ircnn_lstmcell_pa_t_kernel(
 
         const = pool("const", 1)
         wstage = pool("wstage", 2)
-        xg_pool = pool("xg", AHEAD_LOAD_XG + 1)
+        xg_pool = pool("xg", AHEAD_LOAD_XG + 2)
         hx_pool = pool("hx", AHEAD_LOAD_STATE)
         cx_pool = pool("cx", AHEAD_LOAD_STATE + 2)
         pre_pool = pool("pre", AHEAD_BIAS + 2)
@@ -67,13 +69,14 @@ def tile_ircnn_lstmcell_pa_t_kernel(
         cx_v = cx.rearrange("(p s) k -> p s k", s=SLOTS)
         out_v = out.rearrange("(p s) c -> p s c", s=SLOTS)
 
-        hx_sb, cx_sb, xg_sb = {}, {}, {}
-        grouped_sb, codes_sb, scales_sb = {}, {}, {}
-        tr_ps, pre_sb, banks_ps, sig_sb, partner_sb = {}, {}, {}, {}, {}
+        hx_sb, cx_sb, grouped_sb, codes_sb, scales_sb = {}, {}, {}, {}, {}
+        xg_sb, tr_ps, pre_sb, banks_ps, sig_sb, partner_sb = {}, {}, {}, {}, {}, {}
 
-        def load_xg(c):
-            xg_sb[c] = xg_pool.tile([P, CHUNK, GATES * OUT], BF16, name="xg_sb")
-            nc.sync.dma_start(out=xg_sb[c][:], in_=xg_v[:, c * CHUNK : (c + 1) * CHUNK, :])
+        def load_xg(s):
+            xg_sb[s] = xg_pool.tile([P, GATES, OUT], BF16, name="xg_sb")
+            nc.sync.dma_start(
+                out=xg_sb[s][:], in_=xg_v[:, s, :].rearrange("p (g c) -> p g c", g=GATES)
+            )
 
         def load_state(c):
             hx_sb[c] = hx_pool.tile([P, CHUNK, K], BF16, name="hx_sb")
@@ -85,17 +88,6 @@ def tile_ircnn_lstmcell_pa_t_kernel(
             words = rows_bf16.bitcast(F32)
             for u in range(HALVES):
                 nc.tensor.transpose(dst[:, u, :], words[:, u * P : (u + 1) * P], ident[:])
-
-        def stage_bias(s):
-            c, i = divmod(s, CHUNK)
-            pre_sb[s] = pre_pool.tile([P, GATES, OUT], F32, name="pre")
-            for g in range(GATES):
-                nc.vector.tensor_tensor(
-                    out=pre_sb[s][:, g, :],
-                    in0=bias_ps[g][:],
-                    in1=xg_sb[c][:, i, g * OUT : (g + 1) * OUT],
-                    op=ALU.add,
-                )
 
         def stage_transpose(s):
             c, i = divmod(s, CHUNK)
@@ -120,6 +112,13 @@ def tile_ircnn_lstmcell_pa_t_kernel(
                     out=codes_sb[c][:].rearrange("p i o r -> p (i o r)").bitcast(FP8X4),
                     scales=scales_sb[c][:].rearrange("p i o r -> p (i o r)"),
                     in_=grouped_sb[c][:].rearrange("p i o r t -> p (i o r t)"),
+                )
+
+        def stage_bias(s):
+            pre_sb[s] = pre_pool.tile([P, GATES, OUT], F32, name="pre")
+            for g in range(GATES):
+                nc.vector.tensor_tensor(
+                    out=pre_sb[s][:, g, :], in0=bias_ps[g][:], in1=xg_sb[s][:, g, :], op=ALU.add
                 )
 
         def mx_pass(bank, s, operand, m, start, stop):
@@ -156,10 +155,6 @@ def tile_ircnn_lstmcell_pa_t_kernel(
 
         def stage_gates(s):
             c, i = divmod(s, CHUNK)
-            sig_sb[s] = gate_pool.tile([P, 2, OUT], F32, name="sig")
-            nc.scalar.activation(out=sig_sb[s][:], in_=pre_sb[s][:, 0:2, :], func=ACT.Sigmoid)
-            cand = gate_pool.tile([P, OUT], F32)
-            nc.scalar.activation(out=cand[:], in_=pre_sb[s][:, 2, :], func=ACT.Tanh)
             partner_sb[s] = gate_pool.tile([P, 2, OUT], F32, name="partner")
             nc.scalar.activation(
                 out=partner_sb[s][:, 1, :],
@@ -167,39 +162,39 @@ def tile_ircnn_lstmcell_pa_t_kernel(
                 func=ACT.Copy,
                 scale=decay[:, 0, s : s + 1],
             )
+            sig_sb[s] = gate_pool.tile([P, 2, OUT], F32, name="sig")
+            nc.scalar.activation(out=sig_sb[s][:], in_=pre_sb[s][:, 0:2, :], func=ACT.Sigmoid)
+            cand = gate_pool.tile([P, OUT], F32)
+            nc.scalar.activation(out=cand[:], in_=pre_sb[s][:, 2, :], func=ACT.Tanh)
             nc.scalar.activation(
                 out=partner_sb[s][:, 0, :], in_=cand[:], func=ACT.Copy, scale=decay[:, 1, s : s + 1]
             )
 
         def stage_combine(s):
+            engine = nc.vector if s % VECTOR_EVERY == VECTOR_EVERY - 1 else nc.gpsimd
             prod = prod_pool.tile([P, 2, OUT], F32)
-            nc.gpsimd.tensor_tensor(
-                out=prod[:], in0=sig_sb[s][:], in1=partner_sb[s][:], op=ALU.mult
-            )
+            engine.tensor_tensor(out=prod[:], in0=sig_sb[s][:], in1=partner_sb[s][:], op=ALU.mult)
             out_sb = store_pool.tile([P, OUT], F32)
-            nc.gpsimd.tensor_tensor(
-                out=out_sb[:], in0=prod[:, 0, :], in1=prod[:, 1, :], op=ALU.add
-            )
+            engine.tensor_tensor(out=out_sb[:], in0=prod[:, 0, :], in1=prod[:, 1, :], op=ALU.add)
             nc.sync.dma_start(out=out_v[:, s, :], in_=out_sb[:])
 
         bias_row = const.tile([P, GATES * OUT], BF16)
         nc.vector.memset(bias_row[:], 0.0)
         nc.scalar.dma_start(out=bias_row[0:1, :], in_=b_hh.rearrange("(o n) -> o n", o=1))
-        td_bf = const.tile([P, 2, SLOTS], BF16)
-        nc.scalar.dma_start(out=td_bf[:, 0, :], in_=td0.rearrange("(p s) -> p s", s=SLOTS))
-        nc.scalar.dma_start(out=td_bf[:, 1, :], in_=td1.rearrange("(p s) -> p s", s=SLOTS))
         a_bf = const.tile([P, 1], BF16)
         nc.scalar.dma_start(out=a_bf[:], in_=a.partition_broadcast(P))
         b_bf = const.tile([P, 1], BF16)
         nc.scalar.dma_start(out=b_bf[:], in_=b.partition_broadcast(P))
+        td_bf = const.tile([P, 2, SLOTS], BF16)
+        nc.scalar.dma_start(out=td_bf[:, 0, :], in_=td0.rearrange("(p s) -> p s", s=SLOTS))
+        nc.scalar.dma_start(out=td_bf[:, 1, :], in_=td1.rearrange("(p s) -> p s", s=SLOTS))
         ones = const.tile([P, P], BF16)
         nc.vector.memset(ones[:], 1.0)
         ident = const.tile([P, P], F32)
         make_identity(nc, ident[:])
 
-        load_xg(0)
         load_state(0)
-
+        load_xg(0)
         w_hh_v = w_hh.rearrange("(g j p) k -> g p j k", g=GATES, p=P)
         w_views = {
             HH_I: w_hh_v[0],
@@ -212,44 +207,11 @@ def tile_ircnn_lstmcell_pa_t_kernel(
         for m in range(N_WEIGHTS):
             w_raw[m] = const.tile([P, W_TILES, K], BF16, name="w_raw%d" % m)
             nc.sync.dma_start(out=w_raw[m][:], in_=w_views[m])
-        for c in range(1, AHEAD_LOAD_STATE):
+        load_state(1)
+        for s in range(1, AHEAD_LOAD_XG):
+            load_xg(s)
+        for c in range(2, AHEAD_LOAD_STATE):
             load_state(c)
-            if c < AHEAD_LOAD_XG:
-                load_xg(c)
-
-        bias_ps = []
-        for g in range(GATES):
-            bias_bank = psum_bias.tile([P, OUT], F32, name="bias_bank%d" % g)
-            nc.tensor.matmul(
-                out=bias_bank[:],
-                lhsT=ones[:],
-                rhs=bias_row[:, g * OUT : (g + 1) * OUT],
-                start=True,
-                stop=True,
-            )
-            bias_ps.append(bias_bank)
-
-        w_codes = const.tile([P, N_WEIGHTS, OUT], U32, align_bytes=64)
-        w_scales = const.tile([P, N_WEIGHTS, OUT], U8, align_bytes=64)
-        for m in range(N_WEIGHTS):
-            if m < AHEAD_BIAS:
-                stage_bias(m)
-            w_grouped = wstage.tile([P, OUT, PACK], BF16, align_bytes=64)
-            w_grouped_words = w_grouped[:].bitcast(F32)
-            for pair in range(W_TILES // 2):
-                tr = psum_tr.tile([P, 2, HALVES, P], F32, name="tr")
-                for jj in range(2):
-                    transpose_words(tr[:, jj], w_raw[m][:, 2 * pair + jj, :])
-                cols = slice(2 * pair * P, (2 * pair + 2) * P)
-                nc.scalar.copy(
-                    out=w_grouped_words[:, cols, :].rearrange("p (j n) u -> p j n u", j=2),
-                    in_=tr[:].rearrange("p j u n -> p j n u"),
-                )
-            nc.vector.quantize_mx(
-                out=w_codes[:, m, :].bitcast(FP8X4),
-                scales=w_scales[:, m, :],
-                in_=w_grouped[:].rearrange("p n t -> p (n t)"),
-            )
 
         neg_b = const.tile([P, 1], F32)
         nc.vector.tensor_scalar(
@@ -263,27 +225,67 @@ def tile_ircnn_lstmcell_pa_t_kernel(
         nc.vector.tensor_scalar(
             out=decay[:], in0=decay_exp[:], scalar1=a_f32[:, 0:1], scalar2=None, op0=ALU.mult
         )
+        table_warmer = const.tile([P, 1], F32)
+        nc.scalar.activation(out=table_warmer[:], in_=neg_b[:], func=ACT.Sigmoid)
 
-        def in_range(s):
-            return 0 <= s < SLOTS
+        bias_ps = []
+        for g in range(GATES):
+            bias_bank = psum_bias.tile([P, OUT], F32, name="bias_bank%d" % g)
+            nc.tensor.matmul(
+                out=bias_bank[:],
+                lhsT=ones[:],
+                rhs=bias_row[:, g * OUT : (g + 1) * OUT],
+                start=True,
+                stop=True,
+            )
+            bias_ps.append(bias_bank)
 
-        for step in range(-AHEAD_TRANSPOSE, SLOTS + BEHIND_COMBINE):
-            if step >= 0 and step % CHUNK == 0:
-                if step // CHUNK + AHEAD_LOAD_STATE < N_CHUNKS:
-                    load_state(step // CHUNK + AHEAD_LOAD_STATE)
-                if step // CHUNK + AHEAD_LOAD_XG < N_CHUNKS:
-                    load_xg(step // CHUNK + AHEAD_LOAD_XG)
-            if in_range(step):
+        stage_bias(0)
+        for s in range(CHUNK):
+            stage_transpose(s)
+            stage_copy(s)
+
+        w_codes = const.tile([P, N_WEIGHTS, OUT], U32, align_bytes=64)
+        w_scales = const.tile([P, N_WEIGHTS, OUT], U8, align_bytes=64)
+        for m in range(N_WEIGHTS):
+            w_grouped = wstage.tile([P, OUT, PACK], BF16, align_bytes=64)
+            w_grouped_words = w_grouped[:].bitcast(F32)
+            for pair in range(W_TILES // 2):
+                tr = psum_tr.tile([P, 2, HALVES, P], F32, name="tr")
+                for jj in range(2):
+                    transpose_words(tr[:, jj], w_raw[m][:, 2 * pair + jj, :])
+                cols = slice(2 * pair * P, (2 * pair + 2) * P)
+                dst = w_grouped_words[:, cols, :].rearrange("p (j n) u -> p j n u", j=2)
+                src = tr[:].rearrange("p j u n -> p j n u")
+                if pair == 0:
+                    nc.scalar.copy(out=dst, in_=src)
+                else:
+                    nc.vector.tensor_copy(out=dst, in_=src)
+            nc.vector.quantize_mx(
+                out=w_codes[:, m, :].bitcast(FP8X4),
+                scales=w_scales[:, m, :],
+                in_=w_grouped[:].rearrange("p n t -> p (n t)"),
+            )
+
+        def due(s, first=0):
+            return first <= s < SLOTS
+
+        for step in range(CHUNK - AHEAD_TRANSPOSE, SLOTS + BEHIND_COMBINE):
+            if due(step + AHEAD_LOAD_XG, AHEAD_LOAD_XG):
+                load_xg(step + AHEAD_LOAD_XG)
+            if step >= 0 and step % CHUNK == 0 and step // CHUNK + AHEAD_LOAD_STATE < N_CHUNKS:
+                load_state(step // CHUNK + AHEAD_LOAD_STATE)
+            if due(step):
                 stage_sum(step)
-            if in_range(step + AHEAD_COPY):
+            if due(step + AHEAD_COPY, CHUNK):
                 stage_copy(step + AHEAD_COPY)
-            if in_range(step + AHEAD_MATMUL):
+            if due(step + AHEAD_MATMUL):
                 stage_matmul(step + AHEAD_MATMUL)
-            if in_range(step + AHEAD_TRANSPOSE):
+            if due(step + AHEAD_TRANSPOSE, CHUNK):
                 stage_transpose(step + AHEAD_TRANSPOSE)
-            if step >= 0 and in_range(step + AHEAD_BIAS):
+            if due(step + AHEAD_BIAS, 1):
                 stage_bias(step + AHEAD_BIAS)
-            if in_range(step):
+            if due(step):
                 stage_gates(step)
-            if in_range(step - BEHIND_COMBINE):
+            if due(step - BEHIND_COMBINE):
                 stage_combine(step - BEHIND_COMBINE)

@@ -16,14 +16,21 @@ B = 4096
 K = 512
 OUT = 512
 GATES = 3
+IN_GATE, FORGET_GATE, CANDIDATE = 0, 1, 2
+SIGMOIDS = 2
 PACK = 4
+MX_ALIGN = 64
 HALVES = 2
 SLOTS = B // P
 CHUNK = 4
 N_CHUNKS = SLOTS // CHUNK
 W_TILES = OUT // P
+BANK_TILES = 2
+STATES = 2
 HX, CX = 0, 1
-HH_I, P_I, HH_F, P_F, HH_G = 0, 1, 2, 3, 4
+DECAYS = 2
+FORCOFF, INCOFF = 0, 1
+HH_I, PEEP_I, HH_F, PEEP_F, HH_G = 0, 1, 2, 3, 4
 N_WEIGHTS = 5
 
 AHEAD_TRANSPOSE = 7
@@ -36,7 +43,9 @@ AHEAD_LOAD_STATE = 3
 
 VECTOR_EVERY = 16
 
-FLOPS = 2 * B * K * (GATES * OUT + 2 * OUT)
+DOUBLE = 2
+
+FLOPS = 2 * B * K * (GATES * OUT + SIGMOIDS * OUT)
 
 
 def tile_ircnn_lstmcell_pa_t_kernel(
@@ -50,18 +59,18 @@ def tile_ircnn_lstmcell_pa_t_kernel(
             return ctx.enter_context(tc.tile_pool(name=name, bufs=bufs))
 
         const = pool("const", 1)
-        wstage = pool("wstage", 2)
+        wstage = pool("wstage", DOUBLE)
         xg_pool = pool("xg", AHEAD_LOAD_XG + 2)
         hx_pool = pool("hx", AHEAD_LOAD_STATE)
         cx_pool = pool("cx", AHEAD_LOAD_STATE + 2)
         pre_pool = pool("pre", AHEAD_BIAS + 2)
-        grouped_pool = pool("grouped", 2)
-        packed_pool = pool("packed", 2)
+        grouped_pool = pool("grouped", DOUBLE)
+        packed_pool = pool("packed", DOUBLE)
         gate_pool = pool("gate", BEHIND_COMBINE + 2)
-        prod_pool = pool("prod", 2)
-        store_pool = pool("store", 4)
+        prod_pool = pool("prod", DOUBLE)
+        store_pool = pool("store", 2 * DOUBLE)
         psum_bias = ctx.enter_context(tc.psum_pool(name="psum_bias", bufs=1))
-        psum_tr = ctx.enter_context(tc.psum_pool(name="psum_tr", bufs=2))
+        psum_tr = ctx.enter_context(tc.psum_pool(name="psum_tr", bufs=DOUBLE))
         psum_gate = ctx.enter_context(tc.psum_pool(name="psum_gate", bufs=1))
 
         xg_v = xg.rearrange("(p s) c -> p s c", s=SLOTS)
@@ -78,11 +87,12 @@ def tile_ircnn_lstmcell_pa_t_kernel(
                 out=xg_sb[s][:], in_=xg_v[:, s, :].rearrange("p (g c) -> p g c", g=GATES)
             )
 
-        def load_state(c):
-            hx_sb[c] = hx_pool.tile([P, CHUNK, K], BF16, name="hx_sb")
-            nc.sync.dma_start(out=hx_sb[c][:], in_=hx_v[:, c * CHUNK : (c + 1) * CHUNK, :])
-            cx_sb[c] = cx_pool.tile([P, CHUNK, K], BF16, name="cx_sb")
-            nc.sync.dma_start(out=cx_sb[c][:], in_=cx_v[:, c * CHUNK : (c + 1) * CHUNK, :])
+        def load_state(chunk):
+            slots = slice(chunk * CHUNK, (chunk + 1) * CHUNK)
+            hx_sb[chunk] = hx_pool.tile([P, CHUNK, K], BF16, name="hx_sb")
+            nc.sync.dma_start(out=hx_sb[chunk][:], in_=hx_v[:, slots, :])
+            cx_sb[chunk] = cx_pool.tile([P, CHUNK, K], BF16, name="cx_sb")
+            nc.sync.dma_start(out=cx_sb[chunk][:], in_=cx_v[:, slots, :])
 
         def transpose_words(dst, rows_bf16):
             words = rows_bf16.bitcast(F32)
@@ -90,28 +100,32 @@ def tile_ircnn_lstmcell_pa_t_kernel(
                 nc.tensor.transpose(dst[:, u, :], words[:, u * P : (u + 1) * P], ident[:])
 
         def stage_transpose(s):
-            c, i = divmod(s, CHUNK)
-            tr_ps[s] = psum_tr.tile([P, 2, HALVES, P], F32, name="tr")
-            transpose_words(tr_ps[s][:, HX], hx_sb[c][:, i, :])
-            transpose_words(tr_ps[s][:, CX], cx_sb[c][:, i, :])
+            chunk, place = divmod(s, CHUNK)
+            tr_ps[s] = psum_tr.tile([P, STATES, HALVES, P], F32, name="tr")
+            transpose_words(tr_ps[s][:, HX], hx_sb[chunk][:, place, :])
+            transpose_words(tr_ps[s][:, CX], cx_sb[chunk][:, place, :])
 
         def stage_copy(s):
-            c, i = divmod(s, CHUNK)
-            if i == 0:
-                grouped_sb[c] = grouped_pool.tile(
-                    [P, CHUNK, 2, P, PACK], BF16, align_bytes=64, name="grouped"
+            chunk, place = divmod(s, CHUNK)
+            if place == 0:
+                grouped_sb[chunk] = grouped_pool.tile(
+                    [P, CHUNK, STATES, P, PACK], BF16, align_bytes=MX_ALIGN, name="grouped"
                 )
             nc.scalar.copy(
-                out=grouped_sb[c][:, i].bitcast(F32),
+                out=grouped_sb[chunk][:, place].bitcast(F32),
                 in_=tr_ps[s][:].rearrange("p o u r -> p o r u"),
             )
-            if i == CHUNK - 1:
-                codes_sb[c] = packed_pool.tile([P, CHUNK, 2, P], U32, align_bytes=64, name="codes")
-                scales_sb[c] = packed_pool.tile([P, CHUNK, 2, P], U8, align_bytes=64, name="scales")
+            if place == CHUNK - 1:
+                codes_sb[chunk] = packed_pool.tile(
+                    [P, CHUNK, STATES, P], U32, align_bytes=MX_ALIGN, name="codes"
+                )
+                scales_sb[chunk] = packed_pool.tile(
+                    [P, CHUNK, STATES, P], U8, align_bytes=MX_ALIGN, name="scales"
+                )
                 nc.vector.quantize_mx(
-                    out=codes_sb[c][:].rearrange("p i o r -> p (i o r)").bitcast(FP8X4),
-                    scales=scales_sb[c][:].rearrange("p i o r -> p (i o r)"),
-                    in_=grouped_sb[c][:].rearrange("p i o r t -> p (i o r t)"),
+                    out=codes_sb[chunk][:].rearrange("p i o r -> p (i o r)").bitcast(FP8X4),
+                    scales=scales_sb[chunk][:].rearrange("p i o r -> p (i o r)"),
+                    in_=grouped_sb[chunk][:].rearrange("p i o r t -> p (i o r t)"),
                 )
 
         def stage_bias(s):
@@ -121,12 +135,12 @@ def tile_ircnn_lstmcell_pa_t_kernel(
                     out=pre_sb[s][:, g, :], in0=bias_ps[g][:], in1=xg_sb[s][:, g, :], op=ALU.add
                 )
 
-        def mx_pass(bank, s, operand, m, start, stop):
-            c, i = divmod(s, CHUNK)
+        def mx_pass(bank, s, state, m, start, stop):
+            chunk, place = divmod(s, CHUNK)
             nc.tensor.matmul_mx(
                 out=bank[:],
-                lhsT=codes_sb[c][:, i, operand, :].bitcast(FP8X4),
-                lhsT_scale=scales_sb[c][:, i, operand, :],
+                lhsT=codes_sb[chunk][:, place, state, :].bitcast(FP8X4),
+                lhsT_scale=scales_sb[chunk][:, place, state, :],
                 rhs=w_codes[:, m, :].bitcast(FP8X4),
                 rhs_scale=w_scales[:, m, :],
                 start=start,
@@ -136,10 +150,10 @@ def tile_ircnn_lstmcell_pa_t_kernel(
         def stage_matmul(s):
             bank_i = psum_gate.tile([P, OUT], F32)
             mx_pass(bank_i, s, HX, HH_I, True, False)
-            mx_pass(bank_i, s, CX, P_I, False, True)
+            mx_pass(bank_i, s, CX, PEEP_I, False, True)
             bank_f = psum_gate.tile([P, OUT], F32)
             mx_pass(bank_f, s, HX, HH_F, True, False)
-            mx_pass(bank_f, s, CX, P_F, False, True)
+            mx_pass(bank_f, s, CX, PEEP_F, False, True)
             bank_g = psum_gate.tile([P, OUT], F32)
             mx_pass(bank_g, s, HX, HH_G, True, True)
             banks_ps[s] = (bank_i, bank_f, bank_g)
@@ -154,40 +168,55 @@ def tile_ircnn_lstmcell_pa_t_kernel(
                 )
 
         def stage_gates(s):
-            c, i = divmod(s, CHUNK)
-            partner_sb[s] = gate_pool.tile([P, 2, OUT], F32, name="partner")
+            chunk, place = divmod(s, CHUNK)
+            partner_sb[s] = gate_pool.tile([P, SIGMOIDS, OUT], F32, name="partner")
             nc.scalar.activation(
-                out=partner_sb[s][:, 1, :],
-                in_=cx_sb[c][:, i, :],
+                out=partner_sb[s][:, FORGET_GATE, :],
+                in_=cx_sb[chunk][:, place, :],
                 func=ACT.Copy,
-                scale=decay[:, 0, s : s + 1],
+                scale=decay[:, FORCOFF, s : s + 1],
             )
-            sig_sb[s] = gate_pool.tile([P, 2, OUT], F32, name="sig")
-            nc.scalar.activation(out=sig_sb[s][:], in_=pre_sb[s][:, 0:2, :], func=ACT.Sigmoid)
-            cand = gate_pool.tile([P, OUT], F32)
-            nc.scalar.activation(out=cand[:], in_=pre_sb[s][:, 2, :], func=ACT.Tanh)
+            sig_sb[s] = gate_pool.tile([P, SIGMOIDS, OUT], F32, name="sig")
             nc.scalar.activation(
-                out=partner_sb[s][:, 0, :], in_=cand[:], func=ACT.Copy, scale=decay[:, 1, s : s + 1]
+                out=sig_sb[s][:], in_=pre_sb[s][:, 0:SIGMOIDS, :], func=ACT.Sigmoid
+            )
+            cand = gate_pool.tile([P, OUT], F32)
+            nc.scalar.activation(out=cand[:], in_=pre_sb[s][:, CANDIDATE, :], func=ACT.Tanh)
+            nc.scalar.activation(
+                out=partner_sb[s][:, IN_GATE, :],
+                in_=cand[:],
+                func=ACT.Copy,
+                scale=decay[:, INCOFF, s : s + 1],
             )
 
         def stage_combine(s):
             engine = nc.vector if s % VECTOR_EVERY == VECTOR_EVERY - 1 else nc.gpsimd
-            prod = prod_pool.tile([P, 2, OUT], F32)
-            engine.tensor_tensor(out=prod[:], in0=sig_sb[s][:], in1=partner_sb[s][:], op=ALU.mult)
+            prod = prod_pool.tile([P, SIGMOIDS, OUT], F32)
+            for gate in (FORGET_GATE, IN_GATE):
+                engine.tensor_tensor(
+                    out=prod[:, gate, :],
+                    in0=sig_sb[s][:, gate, :],
+                    in1=partner_sb[s][:, gate, :],
+                    op=ALU.mult,
+                )
             out_sb = store_pool.tile([P, OUT], F32)
-            engine.tensor_tensor(out=out_sb[:], in0=prod[:, 0, :], in1=prod[:, 1, :], op=ALU.add)
+            engine.tensor_tensor(
+                out=out_sb[:], in0=prod[:, IN_GATE, :], in1=prod[:, FORGET_GATE, :], op=ALU.add
+            )
             nc.sync.dma_start(out=out_v[:, s, :], in_=out_sb[:])
 
         bias_row = const.tile([P, GATES * OUT], BF16)
         nc.vector.memset(bias_row[:], 0.0)
-        nc.scalar.dma_start(out=bias_row[0:1, :], in_=b_hh.rearrange("(o n) -> o n", o=1))
+        nc.scalar.dma_start(out=bias_row[0:1, :], in_=b_hh.rearrange("(x n) -> x n", x=1))
         a_bf = const.tile([P, 1], BF16)
         nc.scalar.dma_start(out=a_bf[:], in_=a.partition_broadcast(P))
         b_bf = const.tile([P, 1], BF16)
         nc.scalar.dma_start(out=b_bf[:], in_=b.partition_broadcast(P))
-        td_bf = const.tile([P, 2, SLOTS], BF16)
-        nc.scalar.dma_start(out=td_bf[:, 0, :], in_=td0.rearrange("(p s) -> p s", s=SLOTS))
-        nc.scalar.dma_start(out=td_bf[:, 1, :], in_=td1.rearrange("(p s) -> p s", s=SLOTS))
+        td_bf = const.tile([P, DECAYS, SLOTS], BF16)
+        nc.scalar.dma_start(
+            out=td_bf[:, FORCOFF, :], in_=td0.rearrange("(p s) -> p s", s=SLOTS)
+        )
+        nc.scalar.dma_start(out=td_bf[:, INCOFF, :], in_=td1.rearrange("(p s) -> p s", s=SLOTS))
         ones = const.tile([P, P], BF16)
         nc.vector.memset(ones[:], 1.0)
         ident = const.tile([P, P], F32)
@@ -197,11 +226,11 @@ def tile_ircnn_lstmcell_pa_t_kernel(
         load_xg(0)
         w_hh_v = w_hh.rearrange("(g j p) k -> g p j k", g=GATES, p=P)
         w_views = {
-            HH_I: w_hh_v[0],
-            P_I: w_pi.rearrange("(j p) k -> p j k", p=P),
-            HH_F: w_hh_v[1],
-            P_F: w_pf.rearrange("(j p) k -> p j k", p=P),
-            HH_G: w_hh_v[2],
+            HH_I: w_hh_v[IN_GATE],
+            PEEP_I: w_pi.rearrange("(j p) k -> p j k", p=P),
+            HH_F: w_hh_v[FORGET_GATE],
+            PEEP_F: w_pf.rearrange("(j p) k -> p j k", p=P),
+            HH_G: w_hh_v[CANDIDATE],
         }
         w_raw = {}
         for m in range(N_WEIGHTS):
@@ -210,8 +239,8 @@ def tile_ircnn_lstmcell_pa_t_kernel(
         load_state(1)
         for s in range(1, AHEAD_LOAD_XG):
             load_xg(s)
-        for c in range(2, AHEAD_LOAD_STATE):
-            load_state(c)
+        for chunk in range(2, AHEAD_LOAD_STATE):
+            load_state(chunk)
 
         neg_b = const.tile([P, 1], F32)
         nc.vector.tensor_scalar(
@@ -219,9 +248,9 @@ def tile_ircnn_lstmcell_pa_t_kernel(
         )
         a_f32 = const.tile([P, 1], F32)
         nc.vector.tensor_copy(out=a_f32[:], in_=a_bf[:])
-        decay_exp = const.tile([P, 2, SLOTS], F32)
+        decay_exp = const.tile([P, DECAYS, SLOTS], F32)
         nc.scalar.activation(out=decay_exp[:], in_=td_bf[:], func=ACT.Exp, scale=neg_b[:, 0:1])
-        decay = const.tile([P, 2, SLOTS], F32)
+        decay = const.tile([P, DECAYS, SLOTS], F32)
         nc.vector.tensor_scalar(
             out=decay[:], in0=decay_exp[:], scalar1=a_f32[:, 0:1], scalar2=None, op0=ALU.mult
         )
@@ -240,24 +269,25 @@ def tile_ircnn_lstmcell_pa_t_kernel(
             )
             bias_ps.append(bias_bank)
 
-        stage_bias(0)
+        for s in range(AHEAD_BIAS):
+            stage_bias(s)
         for s in range(CHUNK):
             stage_transpose(s)
             stage_copy(s)
 
-        w_codes = const.tile([P, N_WEIGHTS, OUT], U32, align_bytes=64)
-        w_scales = const.tile([P, N_WEIGHTS, OUT], U8, align_bytes=64)
+        w_codes = const.tile([P, N_WEIGHTS, OUT], U32, align_bytes=MX_ALIGN)
+        w_scales = const.tile([P, N_WEIGHTS, OUT], U8, align_bytes=MX_ALIGN)
         for m in range(N_WEIGHTS):
-            w_grouped = wstage.tile([P, OUT, PACK], BF16, align_bytes=64)
+            w_grouped = wstage.tile([P, OUT, PACK], BF16, align_bytes=MX_ALIGN)
             w_grouped_words = w_grouped[:].bitcast(F32)
-            for pair in range(W_TILES // 2):
-                tr = psum_tr.tile([P, 2, HALVES, P], F32, name="tr")
-                for jj in range(2):
-                    transpose_words(tr[:, jj], w_raw[m][:, 2 * pair + jj, :])
-                cols = slice(2 * pair * P, (2 * pair + 2) * P)
-                dst = w_grouped_words[:, cols, :].rearrange("p (j n) u -> p j n u", j=2)
+            for part in range(W_TILES // BANK_TILES):
+                tr = psum_tr.tile([P, BANK_TILES, HALVES, P], F32, name="tr")
+                for j in range(BANK_TILES):
+                    transpose_words(tr[:, j], w_raw[m][:, BANK_TILES * part + j, :])
+                cols = slice(BANK_TILES * part * P, BANK_TILES * (part + 1) * P)
+                dst = w_grouped_words[:, cols, :].rearrange("p (j n) u -> p j n u", j=BANK_TILES)
                 src = tr[:].rearrange("p j u n -> p j n u")
-                if pair == 0:
+                if part == 0:
                     nc.scalar.copy(out=dst, in_=src)
                 else:
                     nc.vector.tensor_copy(out=dst, in_=src)
@@ -283,7 +313,7 @@ def tile_ircnn_lstmcell_pa_t_kernel(
                 stage_matmul(step + AHEAD_MATMUL)
             if due(step + AHEAD_TRANSPOSE, CHUNK):
                 stage_transpose(step + AHEAD_TRANSPOSE)
-            if due(step + AHEAD_BIAS, 1):
+            if due(step + AHEAD_BIAS, AHEAD_BIAS):
                 stage_bias(step + AHEAD_BIAS)
             if due(step):
                 stage_gates(step)

@@ -22,8 +22,7 @@ PACK = 4
 MX_ALIGN = 64
 HALVES = 2
 SLOTS = B // P
-CHUNK = 4
-N_CHUNKS = SLOTS // CHUNK
+LOAD = 4
 W_TILES = OUT // P
 BANK_TILES = 2
 STATES = 2
@@ -33,17 +32,12 @@ FORCOFF, INCOFF = 0, 1
 HH_I, PEEP_I, HH_F, PEEP_F, HH_G = 0, 1, 2, 3, 4
 N_WEIGHTS = 5
 
-AHEAD_TRANSPOSE = 7
-AHEAD_COPY = 6
-AHEAD_MATMUL = 1
-AHEAD_BIAS = 1
-BEHIND_COMBINE = 1
-AHEAD_LOAD_XG = 6
-AHEAD_LOAD_STATE = 3
-
-VECTOR_EVERY = 16
-
-DOUBLE = 2
+LEAD_IF = 7
+LEAD_G = 10
+LEAD_TR = 7
+LOAD_IF_AHEAD = 3
+N_SMALL = 4
+FIRST_STEP = -1
 
 FLOPS = 2 * B * K * (GATES * OUT + SIGMOIDS * OUT)
 
@@ -59,40 +53,68 @@ def tile_ircnn_lstmcell_pa_t_kernel(
             return ctx.enter_context(tc.tile_pool(name=name, bufs=bufs))
 
         const = pool("const", 1)
-        wstage = pool("wstage", DOUBLE)
-        xg_pool = pool("xg", AHEAD_LOAD_XG + 2)
-        hx_pool = pool("hx", AHEAD_LOAD_STATE)
-        cx_pool = pool("cx", AHEAD_LOAD_STATE + 2)
-        pre_pool = pool("pre", AHEAD_BIAS + 2)
-        grouped_pool = pool("grouped", DOUBLE)
-        packed_pool = pool("packed", DOUBLE)
-        gate_pool = pool("gate", BEHIND_COMBINE + 2)
-        prod_pool = pool("prod", DOUBLE)
-        store_pool = pool("store", 2 * DOUBLE)
+        wraw_pool = pool("wraw", 3)
+        wstage = pool("wstage", 2)
+        xgif_pool = pool("xgif", 6)
+        xgg_pool = pool("xgg", 3)
+        hx_pool = pool("hx", 3)
+        cx_pool = pool("cx", 5)
+        preif_pool = pool("preif", LEAD_IF + 3)
+        preg_pool = pool("preg", LEAD_G + 2)
+        grouped_pool = pool("grouped", 2)
+        packed_pool = pool("packed", 2)
+        sig_pool = pool("sig", 3)
+        cand_pool = pool("cand", 2)
+        partner_pool = pool("partner", 3)
+        p1_pool = pool("p1", 3)
+        p2_pool = pool("p2", 3)
+        store_pool = pool("store", 4)
         psum_bias = ctx.enter_context(tc.psum_pool(name="psum_bias", bufs=1))
-        psum_tr = ctx.enter_context(tc.psum_pool(name="psum_tr", bufs=DOUBLE))
+        psum_tr = ctx.enter_context(tc.psum_pool(name="psum_tr", bufs=2))
         psum_gate = ctx.enter_context(tc.psum_pool(name="psum_gate", bufs=1))
+        psum_cx = ctx.enter_context(tc.psum_pool(name="psum_cx", bufs=2))
 
         xg_v = xg.rearrange("(p s) c -> p s c", s=SLOTS)
         hx_v = hx.rearrange("(p s) k -> p s k", s=SLOTS)
         cx_v = cx.rearrange("(p s) k -> p s k", s=SLOTS)
         out_v = out.rearrange("(p s) c -> p s c", s=SLOTS)
 
-        hx_sb, cx_sb, grouped_sb, codes_sb, scales_sb = {}, {}, {}, {}, {}
-        xg_sb, tr_ps, pre_sb, banks_ps, sig_sb, partner_sb = {}, {}, {}, {}, {}, {}
+        chunk_first, chunk_size, chunk_of, place_of = [], [], {}, {}
+        nxt = 0
+        while nxt < SLOTS:
+            size = 2 if len(chunk_first) < N_SMALL else 4
+            for i in range(size):
+                chunk_of[nxt + i] = len(chunk_first)
+                place_of[nxt + i] = i
+            chunk_first.append(nxt)
+            chunk_size.append(size)
+            nxt += size
 
-        def load_xg(s):
-            xg_sb[s] = xg_pool.tile([P, GATES, OUT], BF16, name="xg_sb")
+        def tr_step(s):
+            return max(s - LEAD_TR, (s - 4) // 2)
+
+        hx_sb, cx_sb, xgg_sb, grouped_sb, codes_sb, scales_sb = {}, {}, {}, {}, {}, {}
+        xgif_sb, tr_ps, preif_sb, preg_sb, banks_ps, cx_ps = {}, {}, {}, {}, {}, {}
+        sig_sb, partner_sb, p1_sb, p2_sb = {}, {}, {}, {}
+
+        def load_xgif(s):
+            xgif_sb[s] = xgif_pool.tile([P, SIGMOIDS * OUT], BF16, name="xgif")
+            nc.sync.dma_start(out=xgif_sb[s][:], in_=xg_v[:, s, 0 : SIGMOIDS * OUT])
+
+        def load_xgg(q):
+            xgg_sb[q] = xgg_pool.tile([P, LOAD, OUT], BF16, name="xgg")
             nc.sync.dma_start(
-                out=xg_sb[s][:], in_=xg_v[:, s, :].rearrange("p (g c) -> p g c", g=GATES)
+                out=xgg_sb[q][:],
+                in_=xg_v[:, q * LOAD : (q + 1) * LOAD, SIGMOIDS * OUT : GATES * OUT],
             )
 
-        def load_state(chunk):
-            slots = slice(chunk * CHUNK, (chunk + 1) * CHUNK)
-            hx_sb[chunk] = hx_pool.tile([P, CHUNK, K], BF16, name="hx_sb")
-            nc.sync.dma_start(out=hx_sb[chunk][:], in_=hx_v[:, slots, :])
-            cx_sb[chunk] = cx_pool.tile([P, CHUNK, K], BF16, name="cx_sb")
-            nc.sync.dma_start(out=cx_sb[chunk][:], in_=cx_v[:, slots, :])
+        def load_state(q, lo=0, hi=LOAD):
+            if lo == 0:
+                hx_sb[q] = hx_pool.tile([P, LOAD, K], BF16, name="hx_sb")
+                cx_sb[q] = cx_pool.tile([P, LOAD, K], BF16, name="cx_sb")
+            slots = slice(q * LOAD + lo, q * LOAD + hi)
+            nc.sync.dma_start(out=hx_sb[q][:, lo:hi, :], in_=hx_v[:, slots, :])
+            nc.sync.dma_start(out=cx_sb[q][:, lo:hi, :], in_=cx_v[:, slots, :])
 
         def transpose_words(dst, rows_bf16):
             words = rows_bf16.bitcast(F32)
@@ -100,43 +122,51 @@ def tile_ircnn_lstmcell_pa_t_kernel(
                 nc.tensor.transpose(dst[:, u, :], words[:, u * P : (u + 1) * P], ident[:])
 
         def stage_transpose(s):
-            chunk, place = divmod(s, CHUNK)
+            q, place = divmod(s, LOAD)
             tr_ps[s] = psum_tr.tile([P, STATES, HALVES, P], F32, name="tr")
-            transpose_words(tr_ps[s][:, HX], hx_sb[chunk][:, place, :])
-            transpose_words(tr_ps[s][:, CX], cx_sb[chunk][:, place, :])
+            transpose_words(tr_ps[s][:, HX], hx_sb[q][:, place, :])
+            transpose_words(tr_ps[s][:, CX], cx_sb[q][:, place, :])
 
         def stage_copy(s):
-            chunk, place = divmod(s, CHUNK)
+            chunk, place = chunk_of[s], place_of[s]
             if place == 0:
                 grouped_sb[chunk] = grouped_pool.tile(
-                    [P, CHUNK, STATES, P, PACK], BF16, align_bytes=MX_ALIGN, name="grouped"
+                    [P, chunk_size[chunk], STATES, P, PACK], BF16, align_bytes=MX_ALIGN, name="grouped"
                 )
             nc.scalar.copy(
                 out=grouped_sb[chunk][:, place].bitcast(F32),
                 in_=tr_ps[s][:].rearrange("p o u r -> p o r u"),
             )
-            if place == CHUNK - 1:
-                codes_sb[chunk] = packed_pool.tile(
-                    [P, CHUNK, STATES, P], U32, align_bytes=MX_ALIGN, name="codes"
-                )
-                scales_sb[chunk] = packed_pool.tile(
-                    [P, CHUNK, STATES, P], U8, align_bytes=MX_ALIGN, name="scales"
-                )
-                nc.vector.quantize_mx(
-                    out=codes_sb[chunk][:].rearrange("p i o r -> p (i o r)").bitcast(FP8X4),
-                    scales=scales_sb[chunk][:].rearrange("p i o r -> p (i o r)"),
-                    in_=grouped_sb[chunk][:].rearrange("p i o r t -> p (i o r t)"),
-                )
 
-        def stage_bias(s):
-            pre_sb[s] = pre_pool.tile([P, GATES, OUT], F32, name="pre")
-            for g in range(GATES):
-                nc.vector.tensor_tensor(
-                    out=pre_sb[s][:, g, :], in0=bias_ps[g][:], in1=xg_sb[s][:, g, :], op=ALU.add
-                )
+        def stage_quantise(chunk):
+            size = chunk_size[chunk]
+            codes_sb[chunk] = packed_pool.tile(
+                [P, size, STATES, P], U32, align_bytes=MX_ALIGN, name="codes"
+            )
+            scales_sb[chunk] = packed_pool.tile(
+                [P, size, STATES, P], U8, align_bytes=MX_ALIGN, name="scales"
+            )
+            nc.vector.quantize_mx(
+                out=codes_sb[chunk][:].rearrange("p i o r -> p (i o r)").bitcast(FP8X4),
+                scales=scales_sb[chunk][:].rearrange("p i o r -> p (i o r)"),
+                in_=grouped_sb[chunk][:].rearrange("p i o r t -> p (i o r t)"),
+            )
+
+        def stage_bias_if(s):
+            preif_sb[s] = preif_pool.tile([P, SIGMOIDS * OUT], F32, name="preif")
+            nc.vector.tensor_tensor(
+                out=preif_sb[s][:], in0=bias_if_ps[:], in1=xgif_sb[s][:], op=ALU.add
+            )
+
+        def stage_bias_g(s):
+            q, place = divmod(s, LOAD)
+            preg_sb[s] = preg_pool.tile([P, OUT], F32, name="preg")
+            nc.gpsimd.tensor_tensor(
+                out=preg_sb[s][:], in0=xgg_sb[q][:, place, :], in1=bias_g_sb[:], op=ALU.add
+            )
 
         def mx_pass(bank, s, state, m, start, stop):
-            chunk, place = divmod(s, CHUNK)
+            chunk, place = chunk_of[s], place_of[s]
             nc.tensor.matmul_mx(
                 out=bank[:],
                 lhsT=codes_sb[chunk][:, place, state, :].bitcast(FP8X4),
@@ -147,62 +177,75 @@ def tile_ircnn_lstmcell_pa_t_kernel(
                 stop=stop,
             )
 
-        def stage_matmul(s):
-            bank_i = psum_gate.tile([P, OUT], F32)
-            mx_pass(bank_i, s, HX, HH_I, True, False)
-            mx_pass(bank_i, s, CX, PEEP_I, False, True)
-            bank_f = psum_gate.tile([P, OUT], F32)
-            mx_pass(bank_f, s, HX, HH_F, True, False)
-            mx_pass(bank_f, s, CX, PEEP_F, False, True)
-            bank_g = psum_gate.tile([P, OUT], F32)
-            mx_pass(bank_g, s, HX, HH_G, True, True)
-            banks_ps[s] = (bank_i, bank_f, bank_g)
+        def stage_matmul(s, gate):
+            if gate == IN_GATE:
+                bank_i = psum_gate.tile([P, OUT], F32)
+                mx_pass(bank_i, s, HX, HH_I, True, False)
+                mx_pass(bank_i, s, CX, PEEP_I, False, True)
+                banks_ps[(s, gate)] = bank_i
+            elif gate == FORGET_GATE:
+                bank_f = psum_gate.tile([P, OUT], F32)
+                mx_pass(bank_f, s, HX, HH_F, True, False)
+                mx_pass(bank_f, s, CX, PEEP_F, False, True)
+                banks_ps[(s, gate)] = bank_f
+            else:
+                bank_g = psum_gate.tile([P, OUT], F32)
+                mx_pass(bank_g, s, HX, HH_G, True, True)
+                banks_ps[(s, gate)] = bank_g
 
-        def stage_sum(s):
-            for g in range(GATES):
-                nc.vector.tensor_tensor(
-                    out=pre_sb[s][:, g, :],
-                    in0=banks_ps[s][g][:],
-                    in1=pre_sb[s][:, g, :],
-                    op=ALU.add,
-                )
-
-        def stage_gates(s):
-            chunk, place = divmod(s, CHUNK)
-            partner_sb[s] = gate_pool.tile([P, SIGMOIDS, OUT], F32, name="partner")
-            nc.scalar.activation(
-                out=partner_sb[s][:, FORGET_GATE, :],
-                in_=cx_sb[chunk][:, place, :],
-                func=ACT.Copy,
-                scale=decay[:, FORCOFF, s : s + 1],
-            )
-            sig_sb[s] = gate_pool.tile([P, SIGMOIDS, OUT], F32, name="sig")
-            nc.scalar.activation(
-                out=sig_sb[s][:], in_=pre_sb[s][:, 0:SIGMOIDS, :], func=ACT.Sigmoid
-            )
-            cand = gate_pool.tile([P, OUT], F32)
-            nc.scalar.activation(out=cand[:], in_=pre_sb[s][:, CANDIDATE, :], func=ACT.Tanh)
-            nc.scalar.activation(
-                out=partner_sb[s][:, IN_GATE, :],
-                in_=cand[:],
-                func=ACT.Copy,
-                scale=decay[:, INCOFF, s : s + 1],
+        def stage_cx_psum(s):
+            q, place = divmod(s, LOAD)
+            cx_ps[s] = psum_cx.tile([P, OUT], F32, name="cx_ps")
+            nc.tensor.matmul(
+                out=cx_ps[s][:], lhsT=ident_bf[:], rhs=cx_sb[q][:, place, :], start=True, stop=True
             )
 
-        def stage_combine(s):
-            engine = nc.vector if s % VECTOR_EVERY == VECTOR_EVERY - 1 else nc.gpsimd
-            prod = prod_pool.tile([P, SIGMOIDS, OUT], F32)
-            for gate in (FORGET_GATE, IN_GATE):
-                engine.tensor_tensor(
-                    out=prod[:, gate, :],
-                    in0=sig_sb[s][:, gate, :],
-                    in1=partner_sb[s][:, gate, :],
-                    op=ALU.mult,
-                )
+        def pre_of(s, gate):
+            if gate == CANDIDATE:
+                return preg_sb[s][:]
+            return preif_sb[s][:, gate * OUT : (gate + 1) * OUT]
+
+        def stage_sum(s, gate):
+            nc.vector.tensor_tensor(
+                out=pre_of(s, gate), in0=banks_ps[(s, gate)][:], in1=pre_of(s, gate), op=ALU.add
+            )
+
+        def stage_sigmoid(s):
+            sig_sb[s] = sig_pool.tile([P, SIGMOIDS * OUT], F32, name="sig")
+            nc.scalar.activation(out=sig_sb[s][:], in_=preif_sb[s][:], func=ACT.Sigmoid)
+
+        def stage_tanh(s):
+            cand = cand_pool.tile([P, OUT], F32)
+            nc.scalar.activation(out=cand[:], in_=preg_sb[s][:], func=ACT.Tanh)
+            partner_sb[s] = partner_pool.tile([P, OUT], F32, name="partner")
+            nc.scalar.activation(
+                out=partner_sb[s][:], in_=cand[:], func=ACT.Copy, scale=decay[:, INCOFF, s : s + 1]
+            )
+
+        def stage_p1(s):
+            p1_sb[s] = p1_pool.tile([P, OUT], F32, name="p1")
+            nc.vector.scalar_tensor_tensor(
+                out=p1_sb[s][:],
+                in0=sig_sb[s][:, FORGET_GATE * OUT : (FORGET_GATE + 1) * OUT],
+                scalar=decay[:, FORCOFF, s : s + 1],
+                in1=cx_ps[s][:],
+                op0=ALU.mult,
+                op1=ALU.mult,
+            )
+
+        def stage_p2(s):
+            p2_sb[s] = p2_pool.tile([P, OUT], F32, name="p2")
+            nc.gpsimd.tensor_tensor(
+                out=p2_sb[s][:],
+                in0=sig_sb[s][:, IN_GATE * OUT : (IN_GATE + 1) * OUT],
+                in1=partner_sb[s][:],
+                op=ALU.mult,
+            )
+
+        def stage_add(s):
+            engine = nc.vector if s == SLOTS - 1 else nc.gpsimd
             out_sb = store_pool.tile([P, OUT], F32)
-            engine.tensor_tensor(
-                out=out_sb[:], in0=prod[:, IN_GATE, :], in1=prod[:, FORGET_GATE, :], op=ALU.add
-            )
+            engine.tensor_tensor(out=out_sb[:], in0=p1_sb[s][:], in1=p2_sb[s][:], op=ALU.add)
             nc.sync.dma_start(out=out_v[:, s, :], in_=out_sb[:])
 
         bias_row = const.tile([P, GATES * OUT], BF16)
@@ -213,17 +256,15 @@ def tile_ircnn_lstmcell_pa_t_kernel(
         b_bf = const.tile([P, 1], BF16)
         nc.scalar.dma_start(out=b_bf[:], in_=b.partition_broadcast(P))
         td_bf = const.tile([P, DECAYS, SLOTS], BF16)
-        nc.scalar.dma_start(
-            out=td_bf[:, FORCOFF, :], in_=td0.rearrange("(p s) -> p s", s=SLOTS)
-        )
+        nc.scalar.dma_start(out=td_bf[:, FORCOFF, :], in_=td0.rearrange("(p s) -> p s", s=SLOTS))
         nc.scalar.dma_start(out=td_bf[:, INCOFF, :], in_=td1.rearrange("(p s) -> p s", s=SLOTS))
         ones = const.tile([P, P], BF16)
         nc.vector.memset(ones[:], 1.0)
         ident = const.tile([P, P], F32)
         make_identity(nc, ident[:])
+        ident_bf = const.tile([P, P], BF16)
+        make_identity(nc, ident_bf[:])
 
-        load_state(0)
-        load_xg(0)
         w_hh_v = w_hh.rearrange("(g j p) k -> g p j k", g=GATES, p=P)
         w_views = {
             HH_I: w_hh_v[IN_GATE],
@@ -233,19 +274,37 @@ def tile_ircnn_lstmcell_pa_t_kernel(
             HH_G: w_hh_v[CANDIDATE],
         }
         w_raw = {}
-        for m in range(N_WEIGHTS):
-            w_raw[m] = const.tile([P, W_TILES, K], BF16, name="w_raw%d" % m)
+
+        def load_w(m):
+            w_raw[m] = wraw_pool.tile([P, W_TILES, K], BF16, name="w_raw")
             nc.sync.dma_start(out=w_raw[m][:], in_=w_views[m])
-        load_state(1)
-        for s in range(1, AHEAD_LOAD_XG):
-            load_xg(s)
-        for chunk in range(2, AHEAD_LOAD_STATE):
-            load_state(chunk)
+
+        load_xgg(0)
+        load_xgif(0)
+        load_xgif(1)
+        load_w(0)
+        load_w(1)
+        load_xgif(2)
+        load_state(0, 0, 2)
+        load_xgg(1)
+        load_w(2)
+        load_xgif(3)
+        load_w(3)
+        load_xgif(4)
+        load_w(4)
+        load_xgif(5)
+        load_state(0, 2, 4)
+        load_xgg(2)
+        load_xgif(6)
+        load_state(1, 0, 2)
+        load_xgif(7)
+        load_state(1, 2, 4)
+        load_xgif(8)
+        load_state(2)
+        load_xgg(3)
 
         neg_b = const.tile([P, 1], F32)
-        nc.vector.tensor_scalar(
-            out=neg_b[:], in0=b_bf[:], scalar1=-1.0, scalar2=None, op0=ALU.mult
-        )
+        nc.vector.tensor_scalar(out=neg_b[:], in0=b_bf[:], scalar1=-1.0, scalar2=None, op0=ALU.mult)
         a_f32 = const.tile([P, 1], F32)
         nc.vector.tensor_copy(out=a_f32[:], in_=a_bf[:])
         decay_exp = const.tile([P, DECAYS, SLOTS], F32)
@@ -257,65 +316,117 @@ def tile_ircnn_lstmcell_pa_t_kernel(
         table_warmer = const.tile([P, 1], F32)
         nc.scalar.activation(out=table_warmer[:], in_=neg_b[:], func=ACT.Sigmoid)
 
-        bias_ps = []
-        for g in range(GATES):
-            bias_bank = psum_bias.tile([P, OUT], F32, name="bias_bank%d" % g)
+        bias_if_ps = psum_bias.tile([P, SIGMOIDS * OUT], BF16)
+        bank_g = psum_gate.tile([P, OUT], F32)
+        nc.tensor.matmul(
+            out=bank_g[:], lhsT=ones[:], rhs=bias_row[:, CANDIDATE * OUT : GATES * OUT],
+            start=True, stop=True,
+        )
+        for g in range(SIGMOIDS):
             nc.tensor.matmul(
-                out=bias_bank[:],
+                out=bias_if_ps[:, g * OUT : (g + 1) * OUT],
                 lhsT=ones[:],
                 rhs=bias_row[:, g * OUT : (g + 1) * OUT],
                 start=True,
                 stop=True,
             )
-            bias_ps.append(bias_bank)
+        bias_g_sb = const.tile([P, OUT], F32)
+        nc.scalar.copy(out=bias_g_sb[:], in_=bank_g[:])
 
-        for s in range(AHEAD_BIAS):
-            stage_bias(s)
-        for s in range(CHUNK):
-            stage_transpose(s)
-            stage_copy(s)
+        for s in range(LEAD_G + FIRST_STEP):
+            stage_bias_g(s)
 
         w_codes = const.tile([P, N_WEIGHTS, OUT], U32, align_bytes=MX_ALIGN)
         w_scales = const.tile([P, N_WEIGHTS, OUT], U8, align_bytes=MX_ALIGN)
-        for m in range(N_WEIGHTS):
-            w_grouped = wstage.tile([P, OUT, PACK], BF16, align_bytes=MX_ALIGN)
-            w_grouped_words = w_grouped[:].bitcast(F32)
+        w_grouped = {}
+
+        def weight_turn(m):
+            w_grouped[m] = wstage.tile([P, OUT, PACK], BF16, align_bytes=MX_ALIGN, name="w_grouped")
+            w_grouped_words = w_grouped[m][:].bitcast(F32)
             for part in range(W_TILES // BANK_TILES):
                 tr = psum_tr.tile([P, BANK_TILES, HALVES, P], F32, name="tr")
                 for j in range(BANK_TILES):
                     transpose_words(tr[:, j], w_raw[m][:, BANK_TILES * part + j, :])
                 cols = slice(BANK_TILES * part * P, BANK_TILES * (part + 1) * P)
-                dst = w_grouped_words[:, cols, :].rearrange("p (j n) u -> p j n u", j=BANK_TILES)
-                src = tr[:].rearrange("p j u n -> p j n u")
-                if part == 0:
-                    nc.scalar.copy(out=dst, in_=src)
-                else:
-                    nc.vector.tensor_copy(out=dst, in_=src)
+                nc.scalar.copy(
+                    out=w_grouped_words[:, cols, :].rearrange("p (j n) u -> p j n u", j=BANK_TILES),
+                    in_=tr[:].rearrange("p j u n -> p j n u"),
+                )
+
+        def weight_quantise(m):
             nc.vector.quantize_mx(
                 out=w_codes[:, m, :].bitcast(FP8X4),
                 scales=w_scales[:, m, :],
-                in_=w_grouped[:].rearrange("p n t -> p (n t)"),
+                in_=w_grouped[m][:].rearrange("p n t -> p (n t)"),
             )
+
+        stage_bias_if(0)
+        stage_bias_if(1)
+        weight_turn(0)
+        weight_quantise(0)
+        stage_bias_if(2)
+        weight_turn(1)
+        weight_quantise(1)
+        stage_transpose(0)
+        stage_copy(0)
+        stage_transpose(1)
+        stage_copy(1)
+        stage_bias_if(3)
+        stage_quantise(0)
+        weight_turn(2)
+        weight_quantise(2)
+        stage_bias_if(4)
+        weight_turn(3)
+        weight_quantise(3)
+        stage_bias_if(5)
+        weight_turn(4)
+        weight_quantise(4)
 
         def due(s, first=0):
             return first <= s < SLOTS
 
-        for step in range(CHUNK - AHEAD_TRANSPOSE, SLOTS + BEHIND_COMBINE):
-            if due(step + AHEAD_LOAD_XG, AHEAD_LOAD_XG):
-                load_xg(step + AHEAD_LOAD_XG)
-            if step >= 0 and step % CHUNK == 0 and step // CHUNK + AHEAD_LOAD_STATE < N_CHUNKS:
-                load_state(step // CHUNK + AHEAD_LOAD_STATE)
+        for step in range(FIRST_STEP, SLOTS + 1):
+            s_load = step + LEAD_IF + LOAD_IF_AHEAD
+            if due(s_load, 9):
+                load_xgif(s_load)
+            if (step + LEAD_G + 5) % LOAD == 0 and 4 <= (step + LEAD_G + 5) // LOAD < SLOTS // LOAD:
+                load_xgg((step + LEAD_G + 5) // LOAD)
+            if (step + LEAD_TR + 5) % LOAD == 0 and 3 <= (step + LEAD_TR + 5) // LOAD < SLOTS // LOAD:
+                load_state((step + LEAD_TR + 5) // LOAD)
+
+            copies = [s for s in range(2, SLOTS) if tr_step(s) + 1 == step]
+            for s in copies:
+                stage_copy(s)
             if due(step):
-                stage_sum(step)
-            if due(step + AHEAD_COPY, CHUNK):
-                stage_copy(step + AHEAD_COPY)
-            if due(step + AHEAD_MATMUL):
-                stage_matmul(step + AHEAD_MATMUL)
-            if due(step + AHEAD_TRANSPOSE, CHUNK):
-                stage_transpose(step + AHEAD_TRANSPOSE)
-            if due(step + AHEAD_BIAS, AHEAD_BIAS):
-                stage_bias(step + AHEAD_BIAS)
+                stage_sum(step, IN_GATE)
+            if due(step + 1):
+                stage_matmul(step + 1, IN_GATE)
+            for s in range(2, SLOTS):
+                if tr_step(s) == step:
+                    stage_transpose(s)
+            if due(step + LEAD_IF, LEAD_IF + FIRST_STEP):
+                stage_bias_if(step + LEAD_IF)
             if due(step):
-                stage_gates(step)
-            if due(step - BEHIND_COMBINE):
-                stage_combine(step - BEHIND_COMBINE)
+                stage_sum(step, FORGET_GATE)
+                stage_sigmoid(step)
+            if due(step + 1):
+                stage_matmul(step + 1, FORGET_GATE)
+                stage_cx_psum(step + 1)
+            if due(step - 1):
+                stage_p1(step - 1)
+            if due(step):
+                stage_sum(step, CANDIDATE)
+                stage_tanh(step)
+            if due(step + 1):
+                stage_matmul(step + 1, CANDIDATE)
+            for s in copies:
+                if place_of[s] == chunk_size[chunk_of[s]] - 1:
+                    stage_quantise(chunk_of[s])
+            if due(step - 2) and step - 2 < SLOTS - 1:
+                stage_add(step - 2)
+            if due(step - 1):
+                stage_p2(step - 1)
+            if due(step + LEAD_G, LEAD_G + FIRST_STEP):
+                stage_bias_g(step + LEAD_G)
+            if step - 1 == SLOTS - 1:
+                stage_add(step - 1)

@@ -38,6 +38,7 @@ LEAD_TR = 7
 LOAD_IF_AHEAD = 3
 N_SMALL = 4
 FIRST_STEP = -1
+G_SHARE = 0
 
 FLOPS = 2 * B * K * (GATES * OUT + SIGMOIDS * OUT)
 
@@ -56,7 +57,7 @@ def tile_ircnn_lstmcell_pa_t_kernel(
         wraw_pool = pool("wraw", 3)
         wstage = pool("wstage", 2)
         xgif_pool = pool("xgif", 6)
-        xgg_pool = pool("xgg", 3)
+        xgg_pool = pool("xgg", 4)
         hx_pool = pool("hx", 3)
         cx_pool = pool("cx", 5)
         preif_pool = pool("preif", LEAD_IF + 3)
@@ -72,7 +73,7 @@ def tile_ircnn_lstmcell_pa_t_kernel(
         psum_bias = ctx.enter_context(tc.psum_pool(name="psum_bias", bufs=1))
         psum_tr = ctx.enter_context(tc.psum_pool(name="psum_tr", bufs=2))
         psum_gate = ctx.enter_context(tc.psum_pool(name="psum_gate", bufs=1))
-        psum_cx = ctx.enter_context(tc.psum_pool(name="psum_cx", bufs=2))
+        psum_cx = ctx.enter_context(tc.psum_pool(name="psum_cx", bufs=1))
 
         xg_v = xg.rearrange("(p s) c -> p s c", s=SLOTS)
         hx_v = hx.rearrange("(p s) k -> p s k", s=SLOTS)
@@ -158,12 +159,20 @@ def tile_ircnn_lstmcell_pa_t_kernel(
                 out=preif_sb[s][:], in0=bias_if_ps[:], in1=xgif_sb[s][:], op=ALU.add
             )
 
+        def g_owns(s):
+            return s % 4 < G_SHARE
+
         def stage_bias_g(s):
             q, place = divmod(s, LOAD)
             preg_sb[s] = preg_pool.tile([P, OUT], F32, name="preg")
-            nc.gpsimd.tensor_tensor(
-                out=preg_sb[s][:], in0=xgg_sb[q][:, place, :], in1=bias_g_sb[:], op=ALU.add
-            )
+            if g_owns(s):
+                nc.gpsimd.tensor_tensor(
+                    out=preg_sb[s][:], in0=xgg_sb[q][:, place, :], in1=bias_g_sb[:], op=ALU.add
+                )
+            else:
+                nc.vector.tensor_tensor(
+                    out=preg_sb[s][:], in0=bias_g_ps[:], in1=xgg_sb[q][:, place, :], op=ALU.add
+                )
 
         def mx_pass(bank, s, state, m, start, stop):
             chunk, place = chunk_of[s], place_of[s]
@@ -317,9 +326,9 @@ def tile_ircnn_lstmcell_pa_t_kernel(
         nc.scalar.activation(out=table_warmer[:], in_=neg_b[:], func=ACT.Sigmoid)
 
         bias_if_ps = psum_bias.tile([P, SIGMOIDS * OUT], BF16)
-        bank_g = psum_gate.tile([P, OUT], F32)
+        bias_g_ps = psum_bias.tile([P, OUT], F32)
         nc.tensor.matmul(
-            out=bank_g[:], lhsT=ones[:], rhs=bias_row[:, CANDIDATE * OUT : GATES * OUT],
+            out=bias_g_ps[:], lhsT=ones[:], rhs=bias_row[:, CANDIDATE * OUT : GATES * OUT],
             start=True, stop=True,
         )
         for g in range(SIGMOIDS):
@@ -331,10 +340,16 @@ def tile_ircnn_lstmcell_pa_t_kernel(
                 stop=True,
             )
         bias_g_sb = const.tile([P, OUT], F32)
-        nc.scalar.copy(out=bias_g_sb[:], in_=bank_g[:])
+        nc.scalar.copy(out=bias_g_sb[:], in_=bias_g_ps[:])
 
         for s in range(LEAD_G + FIRST_STEP):
-            stage_bias_g(s)
+            if g_owns(s):
+                stage_bias_g(s)
+
+        def head_bias(s):
+            stage_bias_if(s)
+            if not g_owns(s):
+                stage_bias_g(s)
 
         w_codes = const.tile([P, N_WEIGHTS, OUT], U32, align_bytes=MX_ALIGN)
         w_scales = const.tile([P, N_WEIGHTS, OUT], U8, align_bytes=MX_ALIGN)
@@ -360,25 +375,25 @@ def tile_ircnn_lstmcell_pa_t_kernel(
                 in_=w_grouped[m][:].rearrange("p n t -> p (n t)"),
             )
 
-        stage_bias_if(0)
-        stage_bias_if(1)
+        head_bias(0)
+        head_bias(1)
         weight_turn(0)
         weight_quantise(0)
-        stage_bias_if(2)
+        head_bias(2)
         weight_turn(1)
         weight_quantise(1)
         stage_transpose(0)
         stage_copy(0)
         stage_transpose(1)
         stage_copy(1)
-        stage_bias_if(3)
+        head_bias(3)
         stage_quantise(0)
         weight_turn(2)
         weight_quantise(2)
-        stage_bias_if(4)
+        head_bias(4)
         weight_turn(3)
         weight_quantise(3)
-        stage_bias_if(5)
+        head_bias(5)
         weight_turn(4)
         weight_quantise(4)
 
@@ -411,14 +426,17 @@ def tile_ircnn_lstmcell_pa_t_kernel(
                 stage_sigmoid(step)
             if due(step + 1):
                 stage_matmul(step + 1, FORGET_GATE)
-                stage_cx_psum(step + 1)
             if due(step - 1):
                 stage_p1(step - 1)
+            if due(step):
+                stage_cx_psum(step)
             if due(step):
                 stage_sum(step, CANDIDATE)
                 stage_tanh(step)
             if due(step + 1):
                 stage_matmul(step + 1, CANDIDATE)
+            if due(step + LEAD_IF, LEAD_IF + FIRST_STEP) and not g_owns(step + LEAD_IF):
+                stage_bias_g(step + LEAD_IF)
             for s in copies:
                 if place_of[s] == chunk_size[chunk_of[s]] - 1:
                     stage_quantise(chunk_of[s])
@@ -426,7 +444,7 @@ def tile_ircnn_lstmcell_pa_t_kernel(
                 stage_add(step - 2)
             if due(step - 1):
                 stage_p2(step - 1)
-            if due(step + LEAD_G, LEAD_G + FIRST_STEP):
+            if due(step + LEAD_G, LEAD_G + FIRST_STEP) and g_owns(step + LEAD_G):
                 stage_bias_g(step + LEAD_G)
             if step - 1 == SLOTS - 1:
                 stage_add(step - 1)

@@ -38,7 +38,7 @@ LEAD_TR = 7
 LOAD_IF_AHEAD = 3
 N_SMALL = 4
 FIRST_STEP = -1
-G_SHARE = 0
+G_SLOTS = 16
 
 FLOPS = 2 * B * K * (GATES * OUT + SIGMOIDS * OUT)
 
@@ -160,7 +160,7 @@ def tile_ircnn_lstmcell_pa_t_kernel(
             )
 
         def g_owns(s):
-            return s % 4 < G_SHARE
+            return s < G_SLOTS
 
         def stage_bias_g(s):
             q, place = divmod(s, LOAD)

@@ -38,7 +38,7 @@ LEAD_TR = 7
 LOAD_IF_AHEAD = 3
 N_SMALL = 4
 FIRST_STEP = -1
-G_SLOTS = 16
+G_HEAD = 9
 
 FLOPS = 2 * B * K * (GATES * OUT + SIGMOIDS * OUT)
 
@@ -160,7 +160,7 @@ def tile_ircnn_lstmcell_pa_t_kernel(
             )
 
         def g_owns(s):
-            return s < G_SLOTS
+            return s < G_HEAD or s % 2 == 1
 
         def stage_bias_g(s):
             q, place = divmod(s, LOAD)
@@ -435,8 +435,8 @@ def tile_ircnn_lstmcell_pa_t_kernel(
                 stage_tanh(step)
             if due(step + 1):
                 stage_matmul(step + 1, CANDIDATE)
-            if due(step + LEAD_IF, LEAD_IF + FIRST_STEP) and not g_owns(step + LEAD_IF):
-                stage_bias_g(step + LEAD_IF)
+            if due(step + LEAD_G, LEAD_G + FIRST_STEP) and not g_owns(step + LEAD_G):
+                stage_bias_g(step + LEAD_G)
             for s in copies:
                 if place_of[s] == chunk_size[chunk_of[s]] - 1:
                     stage_quantise(chunk_of[s])

@@ -17,30 +17,29 @@ K = 512
 OUT = 512
 GATES = 3
 IN_GATE, FORGET_GATE, CANDIDATE = 0, 1, 2
-SIGMOIDS = 2
 PACK = 4
 MX_ALIGN = 64
 HALVES = 2
 SLOTS = B // P
 LOAD = 4
+PAIR = 2
 W_TILES = OUT // P
 BANK_TILES = 2
 STATES = 2
 HX, CX = 0, 1
 DECAYS = 2
 FORCOFF, INCOFF = 0, 1
-HH_I, PEEP_I, HH_F, PEEP_F, HH_G = 0, 1, 2, 3, 4
+HH_I, PEEP_I, HH_G, HH_F, PEEP_F = 0, 1, 2, 3, 4
 N_WEIGHTS = 5
+TURNED = 2
+TILES = 4
 
-LEAD_IF = 7
-LEAD_G = 10
-LEAD_TR = 7
-LOAD_IF_AHEAD = 3
-N_SMALL = 4
-FIRST_STEP = -1
-G_HEAD = 9
+LEAD_F = 6
+LOAD_AHEAD = 5
+FIRST_STEP = -7
+W_FIRST_STEP = -5
 
-FLOPS = 2 * B * K * (GATES * OUT + SIGMOIDS * OUT)
+FLOPS = 2 * B * K * (GATES * OUT + 2 * OUT)
 
 
 def tile_ircnn_lstmcell_pa_t_kernel(
@@ -56,151 +55,159 @@ def tile_ircnn_lstmcell_pa_t_kernel(
         const = pool("const", 1)
         wraw_pool = pool("wraw", 3)
         wstage = pool("wstage", 2)
-        xgif_pool = pool("xgif", 6)
-        xgg_pool = pool("xgg", 4)
+        xg_pool = pool("xg", 3)
         hx_pool = pool("hx", 3)
-        cx_pool = pool("cx", 5)
-        preif_pool = pool("preif", LEAD_IF + 3)
-        preg_pool = pool("preg", LEAD_G + 2)
+        cx_pool = pool("cx", 4)
+        pref_pool = pool("pref", LEAD_F + 1)
+        xgt_pool = pool("xgt", 3)
         grouped_pool = pool("grouped", 2)
-        packed_pool = pool("packed", 2)
+        packed_pool = pool("packed", 3)
+        zt_pool = pool("zt", 3)
         sig_pool = pool("sig", 3)
-        cand_pool = pool("cand", 2)
-        partner_pool = pool("partner", 3)
-        p1_pool = pool("p1", 3)
-        p2_pool = pool("p2", 3)
-        store_pool = pool("store", 4)
-        psum_bias = ctx.enter_context(tc.psum_pool(name="psum_bias", bufs=1))
+        p1_pool = pool("p1", 5)
+        p2t_pool = pool("p2t", 4)
+        store_pool = pool("store", 3)
         psum_tr = ctx.enter_context(tc.psum_pool(name="psum_tr", bufs=2))
-        psum_gate = ctx.enter_context(tc.psum_pool(name="psum_gate", bufs=1))
+        psum_f = ctx.enter_context(tc.psum_pool(name="psum_f", bufs=1))
+        psum_z = ctx.enter_context(tc.psum_pool(name="psum_z", bufs=1))
         psum_cx = ctx.enter_context(tc.psum_pool(name="psum_cx", bufs=1))
+        psum_o = ctx.enter_context(tc.psum_pool(name="psum_o", bufs=2))
 
         xg_v = xg.rearrange("(p s) c -> p s c", s=SLOTS)
         hx_v = hx.rearrange("(p s) k -> p s k", s=SLOTS)
         cx_v = cx.rearrange("(p s) k -> p s k", s=SLOTS)
         out_v = out.rearrange("(p s) c -> p s c", s=SLOTS)
 
-        chunk_first, chunk_size, chunk_of, place_of = [], [], {}, {}
-        nxt = 0
-        while nxt < SLOTS:
-            size = 2 if len(chunk_first) < N_SMALL else 4
+        sizes = [2, 2, 2, 2] + [4] * 5 + [2, 1, 1]
+        first_of, size_of, grp_of = [], [], {}
+        for size in sizes:
+            start = sum(size_of)
             for i in range(size):
-                chunk_of[nxt + i] = len(chunk_first)
-                place_of[nxt + i] = i
-            chunk_first.append(nxt)
-            chunk_size.append(size)
-            nxt += size
+                grp_of[start + i] = len(first_of)
+            first_of.append(start)
+            size_of.append(size)
+        assert sum(size_of) == SLOTS
 
         def tr_step(s):
-            return max(s - LEAD_TR, (s - 4) // 2)
+            if s < 2:
+                return FIRST_STEP
+            return max(s - size_of[grp_of[s]] - 2, (s - 2) // 2)
 
-        hx_sb, cx_sb, xgg_sb, grouped_sb, codes_sb, scales_sb = {}, {}, {}, {}, {}, {}
-        xgif_sb, tr_ps, preif_sb, preg_sb, banks_ps, cx_ps = {}, {}, {}, {}, {}, {}
-        sig_sb, partner_sb, p1_sb, p2_sb = {}, {}, {}, {}
+        def q_step(g):
+            return tr_step(first_of[g] + size_of[g] - 1) + 1
 
-        def load_xgif(s):
-            xgif_sb[s] = xgif_pool.tile([P, SIGMOIDS * OUT], BF16, name="xgif")
-            nc.sync.dma_start(out=xgif_sb[s][:], in_=xg_v[:, s, 0 : SIGMOIDS * OUT])
+        def out_step(s):
+            g = grp_of[s]
+            return s + size_of[g] + 1
 
-        def load_xgg(q):
-            xgg_sb[q] = xgg_pool.tile([P, LOAD, OUT], BF16, name="xgg")
-            nc.sync.dma_start(
-                out=xgg_sb[q][:],
-                in_=xg_v[:, q * LOAD : (q + 1) * LOAD, SIGMOIDS * OUT : GATES * OUT],
-            )
+        xg_sb, hx_sb, cx_sb, xgt_sb, grouped_sb, codes_sb, scales_sb = {}, {}, {}, {}, {}, {}, {}
+        pref_sb, bankf_ps, bankz_ps, zt_sb, sig_sb, cx_ps, p1_sb, p2t_sb, banko_ps = (
+            {}, {}, {}, {}, {}, {}, {}, {}, {},
+        )
+        pending = []
 
-        def load_state(q, lo=0, hi=LOAD):
+        def load_pair(h):
+            q, lo = divmod(h * PAIR, LOAD)
             if lo == 0:
+                xg_sb[q] = xg_pool.tile([P, LOAD, GATES * OUT], BF16, name="xg_sb")
                 hx_sb[q] = hx_pool.tile([P, LOAD, K], BF16, name="hx_sb")
                 cx_sb[q] = cx_pool.tile([P, LOAD, K], BF16, name="cx_sb")
-            slots = slice(q * LOAD + lo, q * LOAD + hi)
-            nc.sync.dma_start(out=hx_sb[q][:, lo:hi, :], in_=hx_v[:, slots, :])
-            nc.sync.dma_start(out=cx_sb[q][:, lo:hi, :], in_=cx_v[:, slots, :])
+            slots = slice(h * PAIR, (h + 1) * PAIR)
+            nc.sync.dma_start(out=hx_sb[q][:, lo : lo + PAIR, :], in_=hx_v[:, slots, :])
+            nc.sync.dma_start(out=cx_sb[q][:, lo : lo + PAIR, :], in_=cx_v[:, slots, :])
+            nc.sync.dma_start(out=xg_sb[q][:, lo : lo + PAIR, :], in_=xg_v[:, slots, :])
 
-        def transpose_words(dst, rows_bf16):
-            words = rows_bf16.bitcast(F32)
-            for u in range(HALVES):
-                nc.tensor.transpose(dst[:, u, :], words[:, u * P : (u + 1) * P], ident[:])
+        emitted = [0]
 
-        def stage_transpose(s):
+        def flush(keep=0):
+            while len(pending) - emitted[0] > keep:
+                pending[emitted[0]]()
+                emitted[0] += 1
+
+        def new_tr_bank(shape):
+            flush(keep=1)
+            return psum_tr.tile(shape, F32, name="tr")
+
+        def transpose_words(dst, words):
+            nc.tensor.transpose(dst, words, ident[:])
+
+        def stage_turn_state(s):
             q, place = divmod(s, LOAD)
-            tr_ps[s] = psum_tr.tile([P, STATES, HALVES, P], F32, name="tr")
-            transpose_words(tr_ps[s][:, HX], hx_sb[q][:, place, :])
-            transpose_words(tr_ps[s][:, CX], cx_sb[q][:, place, :])
-
-        def stage_copy(s):
-            chunk, place = chunk_of[s], place_of[s]
-            if place == 0:
-                grouped_sb[chunk] = grouped_pool.tile(
-                    [P, chunk_size[chunk], STATES, P, PACK], BF16, align_bytes=MX_ALIGN, name="grouped"
+            g = grp_of[s]
+            j = s - first_of[g]
+            tr = new_tr_bank([P, STATES, HALVES, P])
+            for o, src in ((HX, hx_sb[q]), (CX, cx_sb[q])):
+                words = src[:, place, :].bitcast(F32)
+                for u in range(HALVES):
+                    transpose_words(tr[:, o, u, :], words[:, u * P : (u + 1) * P])
+            if j == 0:
+                grouped_sb[g] = grouped_pool.tile(
+                    [P, STATES, size_of[g], P, PACK], BF16, align_bytes=MX_ALIGN, name="grouped"
                 )
-            nc.scalar.copy(
-                out=grouped_sb[chunk][:, place].bitcast(F32),
-                in_=tr_ps[s][:].rearrange("p o u r -> p o r u"),
+            dst = grouped_sb[g][:, :, j].bitcast(F32)
+            pending.append(
+                lambda: nc.scalar.copy(out=dst, in_=tr[:].rearrange("p o u r -> p o r u"))
             )
 
-        def stage_quantise(chunk):
-            size = chunk_size[chunk]
-            codes_sb[chunk] = packed_pool.tile(
-                [P, size, STATES, P], U32, align_bytes=MX_ALIGN, name="codes"
-            )
-            scales_sb[chunk] = packed_pool.tile(
-                [P, size, STATES, P], U8, align_bytes=MX_ALIGN, name="scales"
-            )
+        def stage_turn_xg(s):
+            q, place = divmod(s, LOAD)
+            g = grp_of[s]
+            j = s - first_of[g]
+            tr = new_tr_bank([P, TURNED, HALVES, P])
+            words = xg_sb[q][:, place, :].bitcast(F32)
+            for y, gate in enumerate((IN_GATE, CANDIDATE)):
+                for u in range(HALVES):
+                    w0 = gate * (OUT // 2) + u * P
+                    transpose_words(tr[:, y, u, :], words[:, w0 : w0 + P])
+            if j == 0:
+                xgt_sb[g] = xgt_pool.tile([P, size_of[g], TURNED, HALVES, P], F32, name="xgt")
+            dst = xgt_sb[g][:, j]
+            pending.append(lambda: nc.scalar.copy(out=dst, in_=tr[:]))
+
+        def stage_quantise(g):
+            size = size_of[g]
+            codes_sb[g] = packed_pool.tile([P, STATES, size, P], U32, align_bytes=MX_ALIGN, name="codes")
+            scales_sb[g] = packed_pool.tile([P, STATES, size, P], U8, align_bytes=MX_ALIGN, name="scales")
             nc.vector.quantize_mx(
-                out=codes_sb[chunk][:].rearrange("p i o r -> p (i o r)").bitcast(FP8X4),
-                scales=scales_sb[chunk][:].rearrange("p i o r -> p (i o r)"),
-                in_=grouped_sb[chunk][:].rearrange("p i o r t -> p (i o r t)"),
+                out=codes_sb[g][:].rearrange("p o i r -> p (o i r)").bitcast(FP8X4),
+                scales=scales_sb[g][:].rearrange("p o i r -> p (o i r)"),
+                in_=grouped_sb[g][:].rearrange("p o i r t -> p (o i r t)"),
             )
 
-        def stage_bias_if(s):
-            preif_sb[s] = preif_pool.tile([P, SIGMOIDS * OUT], F32, name="preif")
-            nc.vector.tensor_tensor(
-                out=preif_sb[s][:], in0=bias_if_ps[:], in1=xgif_sb[s][:], op=ALU.add
-            )
-
-        def g_owns(s):
-            return s < G_HEAD or s % 2 == 1
-
-        def stage_bias_g(s):
+        def stage_bias_f(s):
             q, place = divmod(s, LOAD)
-            preg_sb[s] = preg_pool.tile([P, OUT], F32, name="preg")
-            if g_owns(s):
-                nc.gpsimd.tensor_tensor(
-                    out=preg_sb[s][:], in0=xgg_sb[q][:, place, :], in1=bias_g_sb[:], op=ALU.add
-                )
-            else:
-                nc.vector.tensor_tensor(
-                    out=preg_sb[s][:], in0=bias_g_ps[:], in1=xgg_sb[q][:, place, :], op=ALU.add
-                )
-
-        def mx_pass(bank, s, state, m, start, stop):
-            chunk, place = chunk_of[s], place_of[s]
-            nc.tensor.matmul_mx(
-                out=bank[:],
-                lhsT=codes_sb[chunk][:, place, state, :].bitcast(FP8X4),
-                lhsT_scale=scales_sb[chunk][:, place, state, :],
-                rhs=w_codes[:, m, :].bitcast(FP8X4),
-                rhs_scale=w_scales[:, m, :],
-                start=start,
-                stop=stop,
+            pref_sb[s] = pref_pool.tile([P, OUT], F32, name="pref")
+            nc.gpsimd.tensor_tensor(
+                out=pref_sb[s][:],
+                in0=xg_sb[q][:, place, FORGET_GATE * OUT : (FORGET_GATE + 1) * OUT],
+                in1=bias_f_sb[:],
+                op=ALU.add,
             )
 
-        def stage_matmul(s, gate):
-            if gate == IN_GATE:
-                bank_i = psum_gate.tile([P, OUT], F32)
-                mx_pass(bank_i, s, HX, HH_I, True, False)
-                mx_pass(bank_i, s, CX, PEEP_I, False, True)
-                banks_ps[(s, gate)] = bank_i
-            elif gate == FORGET_GATE:
-                bank_f = psum_gate.tile([P, OUT], F32)
-                mx_pass(bank_f, s, HX, HH_F, True, False)
-                mx_pass(bank_f, s, CX, PEEP_F, False, True)
-                banks_ps[(s, gate)] = bank_f
-            else:
-                bank_g = psum_gate.tile([P, OUT], F32)
-                mx_pass(bank_g, s, HX, HH_G, True, True)
-                banks_ps[(s, gate)] = bank_g
+        def stage_matmul_f(s):
+            g = grp_of[s]
+            j = s - first_of[g]
+            bank_f = psum_f.tile([P, OUT], F32)
+            for state, m in ((HX, HH_F), (CX, PEEP_F)):
+                nc.tensor.matmul_mx(
+                    out=bank_f[:],
+                    lhsT=codes_sb[g][:, state, j, :].bitcast(FP8X4),
+                    lhsT_scale=scales_sb[g][:, state, j, :],
+                    rhs=w_codes[:, m, :].bitcast(FP8X4),
+                    rhs_scale=w_scales[:, m, :],
+                    start=(state == HX),
+                    stop=(state == CX),
+                )
+            bankf_ps[s] = bank_f
+
+        def stage_sum_f(s):
+            nc.vector.tensor_tensor(
+                out=pref_sb[s][:], in0=bankf_ps[s][:], in1=pref_sb[s][:], op=ALU.add
+            )
+
+        def stage_sigmoid_f(s):
+            sig_sb[s] = sig_pool.tile([P, OUT], F32, name="sig")
+            nc.scalar.activation(out=sig_sb[s][:], in_=pref_sb[s][:], func=ACT.Sigmoid)
 
         def stage_cx_psum(s):
             q, place = divmod(s, LOAD)
@@ -209,57 +216,128 @@ def tile_ircnn_lstmcell_pa_t_kernel(
                 out=cx_ps[s][:], lhsT=ident_bf[:], rhs=cx_sb[q][:, place, :], start=True, stop=True
             )
 
-        def pre_of(s, gate):
-            if gate == CANDIDATE:
-                return preg_sb[s][:]
-            return preif_sb[s][:, gate * OUT : (gate + 1) * OUT]
-
-        def stage_sum(s, gate):
-            nc.vector.tensor_tensor(
-                out=pre_of(s, gate), in0=banks_ps[(s, gate)][:], in1=pre_of(s, gate), op=ALU.add
-            )
-
-        def stage_sigmoid(s):
-            sig_sb[s] = sig_pool.tile([P, SIGMOIDS * OUT], F32, name="sig")
-            nc.scalar.activation(out=sig_sb[s][:], in_=preif_sb[s][:], func=ACT.Sigmoid)
-
-        def stage_tanh(s):
-            cand = cand_pool.tile([P, OUT], F32)
-            nc.scalar.activation(out=cand[:], in_=preg_sb[s][:], func=ACT.Tanh)
-            partner_sb[s] = partner_pool.tile([P, OUT], F32, name="partner")
-            nc.scalar.activation(
-                out=partner_sb[s][:], in_=cand[:], func=ACT.Copy, scale=decay[:, INCOFF, s : s + 1]
-            )
-
         def stage_p1(s):
             p1_sb[s] = p1_pool.tile([P, OUT], F32, name="p1")
             nc.vector.scalar_tensor_tensor(
                 out=p1_sb[s][:],
-                in0=sig_sb[s][:, FORGET_GATE * OUT : (FORGET_GATE + 1) * OUT],
+                in0=sig_sb[s][:],
                 scalar=decay[:, FORCOFF, s : s + 1],
                 in1=cx_ps[s][:],
                 op0=ALU.mult,
                 op1=ALU.mult,
             )
 
-        def stage_p2(s):
-            p2_sb[s] = p2_pool.tile([P, OUT], F32, name="p2")
+        def tiles_of(s):
+            g = grp_of[s]
+            share = TILES // size_of[g]
+            j = s - first_of[g]
+            return list(range(j * share, (j + 1) * share))
+
+        def stage_matmul_t(s, y):
+            g = grp_of[s]
+            width = size_of[g] * P
+            if y == 0:
+                bank_zi = psum_z.tile([P, OUT], F32)
+                bank = bank_zi
+                passes = ((HX, HH_I), (CX, PEEP_I))
+            else:
+                bank_zg = psum_z.tile([P, OUT], F32)
+                bank = bank_zg
+                passes = ((HX, HH_G),)
+            for i, tile_no in enumerate(tiles_of(s)):
+                for state, m in passes:
+                    nc.tensor.matmul_mx(
+                        out=bank[:, i * width : (i + 1) * width],
+                        lhsT=w_codes[:, m, tile_no * P : (tile_no + 1) * P].bitcast(FP8X4),
+                        lhsT_scale=w_scales[:, m, tile_no * P : (tile_no + 1) * P],
+                        rhs=codes_sb[g][:, state].rearrange("p i r -> p (i r)").bitcast(FP8X4),
+                        rhs_scale=scales_sb[g][:, state].rearrange("p i r -> p (i r)"),
+                        start=(state == passes[0][0]),
+                        stop=(state == passes[-1][0]),
+                    )
+            bankz_ps[(s, y)] = bank
+
+        def shaped(ap, size):
+            if size == 4:
+                return ap.rearrange("p (i r) -> p i r", i=4)
+            if size == 2:
+                return ap.rearrange("p (e i r) -> p e i r", e=2, i=2)
+            return ap.rearrange("p (u e r) -> p u e r", u=2, e=2)
+
+        def xg_turned(s, y):
+            g = grp_of[s]
+            size = size_of[g]
+            flat = xgt_sb[g][:].rearrange("p i y u r -> p (i y u r)").bitcast(BF16)
+            v = flat.rearrange("p (i y u r e) -> p i y u r e", i=size, y=TURNED, u=HALVES, e=2)
+            first_tile = tiles_of(s)[0]
+            if size == 4:
+                return v[:, :, y, first_tile // 2, :, first_tile % 2]
+            if size == 2:
+                return v[:, :, y, first_tile // 2, :, :].rearrange("p i r e -> p e i r")
+            return v[:, 0, y].rearrange("p u r e -> p u e r")
+
+        def stage_sum_t(s, y):
+            size = size_of[grp_of[s]]
+            zt_sb[(s, y)] = zt_pool.tile([P, OUT], F32, name="zt%d" % y)
+            nc.vector.tensor_tensor(
+                out=shaped(zt_sb[(s, y)][:], size),
+                in0=shaped(bankz_ps[(s, y)][:], size),
+                in1=xg_turned(s, y),
+                op=ALU.add,
+            )
+
+        def stage_act_t(s, y):
+            width = size_of[grp_of[s]] * P
+            for i, tile_no in enumerate(tiles_of(s)):
+                part = zt_sb[(s, y)][:, i * width : (i + 1) * width]
+                nc.scalar.activation(
+                    out=part,
+                    in_=part,
+                    func=(ACT.Sigmoid if y == 0 else ACT.Tanh),
+                    bias=bias_col[:, y, tile_no : tile_no + 1],
+                )
+
+        def stage_p2t(s):
+            g = grp_of[s]
+            j = s - first_of[g]
+            if j == 0:
+                p2t_sb[g] = p2t_pool.tile([P, TILES * size_of[g] * P], F32, name="p2t")
             nc.gpsimd.tensor_tensor(
-                out=p2_sb[s][:],
-                in0=sig_sb[s][:, IN_GATE * OUT : (IN_GATE + 1) * OUT],
-                in1=partner_sb[s][:],
+                out=p2t_sb[g][:, j * OUT : (j + 1) * OUT],
+                in0=zt_sb[(s, 0)][:],
+                in1=zt_sb[(s, 1)][:],
                 op=ALU.mult,
             )
 
-        def stage_add(s):
-            engine = nc.vector if s == SLOTS - 1 else nc.gpsimd
+        def stage_turn_back(s):
+            g = grp_of[s]
+            j = s - first_of[g]
+            width = size_of[g] * P
+            banko_ps[s] = psum_o.tile([P, 2, HALVES, P], F32, name="bank_o")
+            for tile_no in range(TILES):
+                c0 = tile_no * width + j * P
+                nc.tensor.transpose(
+                    banko_ps[s][:, tile_no % 2, tile_no // 2, :], p2t_sb[g][:, c0 : c0 + P], ident[:]
+                )
+
+        def stage_final(s):
             out_sb = store_pool.tile([P, OUT], F32)
-            engine.tensor_tensor(out=out_sb[:], in0=p1_sb[s][:], in1=p2_sb[s][:], op=ALU.add)
+            nc.vector.scalar_tensor_tensor(
+                out=out_sb[:].rearrange("r (w e) -> r w e", e=2),
+                in0=banko_ps[s][:].rearrange("r e u p -> r (u p) e"),
+                scalar=decay[:, INCOFF, s : s + 1],
+                in1=p1_sb[s][:].rearrange("r (w e) -> r w e", e=2),
+                op0=ALU.mult,
+                op1=ALU.add,
+            )
             nc.sync.dma_start(out=out_v[:, s, :], in_=out_sb[:])
 
-        bias_row = const.tile([P, GATES * OUT], BF16)
+        bias_row = const.tile([P, OUT], BF16)
         nc.vector.memset(bias_row[:], 0.0)
-        nc.scalar.dma_start(out=bias_row[0:1, :], in_=b_hh.rearrange("(x n) -> x n", x=1))
+        nc.scalar.dma_start(
+            out=bias_row[0:1, :],
+            in_=b_hh[FORGET_GATE * OUT : (FORGET_GATE + 1) * OUT].rearrange("(x n) -> x n", x=1),
+        )
         a_bf = const.tile([P, 1], BF16)
         nc.scalar.dma_start(out=a_bf[:], in_=a.partition_broadcast(P))
         b_bf = const.tile([P, 1], BF16)
@@ -267,6 +345,13 @@ def tile_ircnn_lstmcell_pa_t_kernel(
         td_bf = const.tile([P, DECAYS, SLOTS], BF16)
         nc.scalar.dma_start(out=td_bf[:, FORCOFF, :], in_=td0.rearrange("(p s) -> p s", s=SLOTS))
         nc.scalar.dma_start(out=td_bf[:, INCOFF, :], in_=td1.rearrange("(p s) -> p s", s=SLOTS))
+        bias_col_bf = {}
+        for y, gate in enumerate((IN_GATE, CANDIDATE)):
+            bias_col_bf[y] = const.tile([P, HALVES, 2], BF16, name="bias_col_bf%d" % y)
+            nc.scalar.dma_start(
+                out=bias_col_bf[y][:],
+                in_=b_hh[gate * OUT : (gate + 1) * OUT].rearrange("(u p e) -> p u e", u=HALVES, e=2),
+            )
         ones = const.tile([P, P], BF16)
         nc.vector.memset(ones[:], 1.0)
         ident = const.tile([P, P], F32)
@@ -274,43 +359,29 @@ def tile_ircnn_lstmcell_pa_t_kernel(
         ident_bf = const.tile([P, P], BF16)
         make_identity(nc, ident_bf[:])
 
-        w_hh_v = w_hh.rearrange("(g j p) k -> g p j k", g=GATES, p=P)
-        w_views = {
-            HH_I: w_hh_v[IN_GATE],
-            PEEP_I: w_pi.rearrange("(j p) k -> p j k", p=P),
-            HH_F: w_hh_v[FORGET_GATE],
-            PEEP_F: w_pf.rearrange("(j p) k -> p j k", p=P),
-            HH_G: w_hh_v[CANDIDATE],
+        w_hh_g = w_hh.rearrange("(g n) k -> g n k", g=GATES)
+        w_rows = {
+            HH_I: w_hh_g[IN_GATE],
+            PEEP_I: w_pi,
+            HH_G: w_hh_g[CANDIDATE],
+            HH_F: w_hh_g[FORGET_GATE],
+            PEEP_F: w_pf,
         }
         w_raw = {}
 
         def load_w(m):
             w_raw[m] = wraw_pool.tile([P, W_TILES, K], BF16, name="w_raw")
-            nc.sync.dma_start(out=w_raw[m][:], in_=w_views[m])
+            if m in (HH_F, PEEP_F):
+                nc.sync.dma_start(out=w_raw[m][:], in_=w_rows[m].rearrange("(j p) k -> p j k", p=P))
+            else:
+                nc.sync.dma_start(
+                    out=w_raw[m][:].rearrange("p (u e) k -> p u (e k)", e=2),
+                    in_=w_rows[m].rearrange("(u p e) k -> p u (e k)", u=HALVES, e=2),
+                )
 
-        load_xgg(0)
-        load_xgif(0)
-        load_xgif(1)
-        load_w(0)
-        load_w(1)
-        load_xgif(2)
-        load_state(0, 0, 2)
-        load_xgg(1)
-        load_w(2)
-        load_xgif(3)
-        load_w(3)
-        load_xgif(4)
-        load_w(4)
-        load_xgif(5)
-        load_state(0, 2, 4)
-        load_xgg(2)
-        load_xgif(6)
-        load_state(1, 0, 2)
-        load_xgif(7)
-        load_state(1, 2, 4)
-        load_xgif(8)
-        load_state(2)
-        load_xgg(3)
+        load_pair(0)
+        for m in range(N_WEIGHTS):
+            load_w(m)
 
         neg_b = const.tile([P, 1], F32)
         nc.vector.tensor_scalar(out=neg_b[:], in0=b_bf[:], scalar1=-1.0, scalar2=None, op0=ALU.mult)
@@ -324,127 +395,85 @@ def tile_ircnn_lstmcell_pa_t_kernel(
         )
         table_warmer = const.tile([P, 1], F32)
         nc.scalar.activation(out=table_warmer[:], in_=neg_b[:], func=ACT.Sigmoid)
-
-        bias_if_ps = psum_bias.tile([P, SIGMOIDS * OUT], BF16)
-        bias_g_ps = psum_bias.tile([P, OUT], F32)
-        nc.tensor.matmul(
-            out=bias_g_ps[:], lhsT=ones[:], rhs=bias_row[:, CANDIDATE * OUT : GATES * OUT],
-            start=True, stop=True,
-        )
-        for g in range(SIGMOIDS):
-            nc.tensor.matmul(
-                out=bias_if_ps[:, g * OUT : (g + 1) * OUT],
-                lhsT=ones[:],
-                rhs=bias_row[:, g * OUT : (g + 1) * OUT],
-                start=True,
-                stop=True,
+        bias_col = const.tile([P, TURNED, TILES], F32)
+        for y in range(TURNED):
+            nc.vector.tensor_copy(
+                out=bias_col[:, y, :], in_=bias_col_bf[y][:].rearrange("p u e -> p (u e)")
             )
-        bias_g_sb = const.tile([P, OUT], F32)
-        nc.scalar.copy(out=bias_g_sb[:], in_=bias_g_ps[:])
 
-        for s in range(LEAD_G + FIRST_STEP):
-            if g_owns(s):
-                stage_bias_g(s)
-
-        def head_bias(s):
-            stage_bias_if(s)
-            if not g_owns(s):
-                stage_bias_g(s)
+        bank_f = psum_f.tile([P, OUT], F32)
+        nc.tensor.matmul(out=bank_f[:], lhsT=ones[:], rhs=bias_row[:], start=True, stop=True)
+        bias_f_sb = const.tile([P, OUT], F32)
+        nc.scalar.copy(out=bias_f_sb[:], in_=bank_f[:])
 
         w_codes = const.tile([P, N_WEIGHTS, OUT], U32, align_bytes=MX_ALIGN)
         w_scales = const.tile([P, N_WEIGHTS, OUT], U8, align_bytes=MX_ALIGN)
-        w_grouped = {}
 
-        def weight_turn(m):
-            w_grouped[m] = wstage.tile([P, OUT, PACK], BF16, align_bytes=MX_ALIGN, name="w_grouped")
-            w_grouped_words = w_grouped[m][:].bitcast(F32)
+        def stage_weight(m):
+            w_grouped = wstage.tile([P, OUT, PACK], BF16, align_bytes=MX_ALIGN)
+            w_grouped_words = w_grouped[:].bitcast(F32)
             for part in range(W_TILES // BANK_TILES):
-                tr = psum_tr.tile([P, BANK_TILES, HALVES, P], F32, name="tr")
+                tr = new_tr_bank([P, BANK_TILES, HALVES, P])
                 for j in range(BANK_TILES):
-                    transpose_words(tr[:, j], w_raw[m][:, BANK_TILES * part + j, :])
+                    words = w_raw[m][:, BANK_TILES * part + j, :].bitcast(F32)
+                    for u in range(HALVES):
+                        transpose_words(tr[:, j, u, :], words[:, u * P : (u + 1) * P])
                 cols = slice(BANK_TILES * part * P, BANK_TILES * (part + 1) * P)
-                nc.scalar.copy(
-                    out=w_grouped_words[:, cols, :].rearrange("p (j n) u -> p j n u", j=BANK_TILES),
-                    in_=tr[:].rearrange("p j u n -> p j n u"),
-                )
-
-        def weight_quantise(m):
+                dst = w_grouped_words[:, cols, :].rearrange("p (j n) u -> p j n u", j=BANK_TILES)
+                src = tr[:].rearrange("p j u n -> p j n u")
+                if part == 0:
+                    nc.scalar.copy(out=dst, in_=src)
+                else:
+                    nc.vector.tensor_copy(out=dst, in_=src)
             nc.vector.quantize_mx(
                 out=w_codes[:, m, :].bitcast(FP8X4),
                 scales=w_scales[:, m, :],
-                in_=w_grouped[m][:].rearrange("p n t -> p (n t)"),
+                in_=w_grouped[:].rearrange("p n t -> p (n t)"),
             )
 
-        head_bias(0)
-        head_bias(1)
-        weight_turn(0)
-        weight_quantise(0)
-        head_bias(2)
-        weight_turn(1)
-        weight_quantise(1)
-        stage_transpose(0)
-        stage_copy(0)
-        stage_transpose(1)
-        stage_copy(1)
-        head_bias(3)
-        stage_quantise(0)
-        weight_turn(2)
-        weight_quantise(2)
-        head_bias(4)
-        weight_turn(3)
-        weight_quantise(3)
-        head_bias(5)
-        weight_turn(4)
-        weight_quantise(4)
+        def due(s):
+            return 0 <= s < SLOTS
 
-        def due(s, first=0):
-            return first <= s < SLOTS
-
-        for step in range(FIRST_STEP, SLOTS + 1):
-            s_load = step + LEAD_IF + LOAD_IF_AHEAD
-            if due(s_load, 9):
-                load_xgif(s_load)
-            if (step + LEAD_G + 5) % LOAD == 0 and 4 <= (step + LEAD_G + 5) // LOAD < SLOTS // LOAD:
-                load_xgg((step + LEAD_G + 5) // LOAD)
-            if (step + LEAD_TR + 5) % LOAD == 0 and 3 <= (step + LEAD_TR + 5) // LOAD < SLOTS // LOAD:
-                load_state((step + LEAD_TR + 5) // LOAD)
-
-            copies = [s for s in range(2, SLOTS) if tr_step(s) + 1 == step]
-            for s in copies:
-                stage_copy(s)
+        for step in range(FIRST_STEP, SLOTS + 6):
+            flush()
+            for h in range(1, SLOTS // PAIR):
+                if max(tr_step(h * PAIR) - LOAD_AHEAD, FIRST_STEP) == step:
+                    load_pair(h)
+            if 0 <= step - W_FIRST_STEP < N_WEIGHTS:
+                stage_weight(step - W_FIRST_STEP)
+            outs = [s for s in range(SLOTS) if out_step(s) == step]
+            for s in outs[:2]:
+                stage_turn_back(s)
             if due(step):
-                stage_sum(step, IN_GATE)
-            if due(step + 1):
-                stage_matmul(step + 1, IN_GATE)
-            for s in range(2, SLOTS):
-                if tr_step(s) == step:
-                    stage_transpose(s)
-            if due(step + LEAD_IF, LEAD_IF + FIRST_STEP):
-                stage_bias_if(step + LEAD_IF)
-            if due(step):
-                stage_sum(step, FORGET_GATE)
-                stage_sigmoid(step)
-            if due(step + 1):
-                stage_matmul(step + 1, FORGET_GATE)
+                stage_sum_f(step)
+                stage_sigmoid_f(step)
+                stage_sum_t(step, 0)
+                stage_act_t(step, 0)
             if due(step - 1):
                 stage_p1(step - 1)
             if due(step):
-                stage_cx_psum(step)
-            if due(step):
-                stage_sum(step, CANDIDATE)
-                stage_tanh(step)
+                stage_sum_t(step, 1)
+                stage_act_t(step, 1)
+            for i, s in enumerate(outs):
+                if i >= 2:
+                    stage_turn_back(s)
+                stage_final(s)
+            for g in range(len(first_of)):
+                if q_step(g) == step:
+                    stage_quantise(g)
+            for s in range(SLOTS):
+                if tr_step(s) == step:
+                    stage_turn_state(s)
+                    stage_turn_xg(s)
             if due(step + 1):
-                stage_matmul(step + 1, CANDIDATE)
-            if due(step + LEAD_G, LEAD_G + FIRST_STEP) and not g_owns(step + LEAD_G):
-                stage_bias_g(step + LEAD_G)
-            for s in copies:
-                if place_of[s] == chunk_size[chunk_of[s]] - 1:
-                    stage_quantise(chunk_of[s])
-            if due(step - 2) and step - 2 < SLOTS - 1:
-                stage_add(step - 2)
-            if due(step - 1):
-                stage_p2(step - 1)
-            if due(step + LEAD_G, LEAD_G + FIRST_STEP) and g_owns(step + LEAD_G):
-                stage_bias_g(step + LEAD_G)
-            if step - 1 == SLOTS - 1:
-                stage_add(step - 1)
+                stage_matmul_f(step + 1)
+                stage_matmul_t(step + 1, 0)
+            if due(step):
+                stage_cx_psum(step)
+            if due(step + 1):
+                stage_matmul_t(step + 1, 1)
+            if due(step):
+                stage_p2t(step)
+            for s in range(SLOTS):
+                if max(s - LEAD_F, tr_step(s)) == step:
+                    stage_bias_f(s)

@@ -461,13 +461,14 @@ def tile_ircnn_lstmcell_pa_t_kernel(
             for g in range(len(first_of)):
                 if q_step(g) == step:
                     stage_quantise(g)
-            for s in range(SLOTS):
-                if tr_step(s) == step:
-                    stage_turn_state(s)
-                    stage_turn_xg(s)
+            turns = [s for s in range(SLOTS) if tr_step(s) == step]
+            for s in turns:
+                stage_turn_state(s)
             if due(step + 1):
                 stage_matmul_f(step + 1)
                 stage_matmul_t(step + 1, 0)
+            for s in turns:
+                stage_turn_xg(s)
             if due(step):
                 stage_cx_psum(step)
             if due(step + 1):

@@ -78,7 +78,7 @@ def tile_ircnn_lstmcell_pa_t_kernel(
         cx_v = cx.rearrange("(p s) k -> p s k", s=SLOTS)
         out_v = out.rearrange("(p s) c -> p s c", s=SLOTS)
 
-        sizes = [2, 2, 2, 2] + [4] * 5 + [2, 1, 1]
+        sizes = [1, 1, 2, 2, 2] + [4] * 5 + [2, 1, 1]
         first_of, size_of, grp_of = [], [], {}
         for size in sizes:
             start = sum(size_of)
@@ -89,7 +89,7 @@ def tile_ircnn_lstmcell_pa_t_kernel(
         assert sum(size_of) == SLOTS
 
         def tr_step(s):
-            if s < 2:
+            if s < 1:
                 return FIRST_STEP
             return max(s - size_of[grp_of[s]] - 2, (s - 2) // 2)
 
@@ -106,16 +106,19 @@ def tile_ircnn_lstmcell_pa_t_kernel(
         )
         pending = []
 
-        def load_pair(h):
-            q, lo = divmod(h * PAIR, LOAD)
+        def load_slots(s0, count):
+            q, lo = divmod(s0, LOAD)
             if lo == 0:
                 xg_sb[q] = xg_pool.tile([P, LOAD, GATES * OUT], BF16, name="xg_sb")
                 hx_sb[q] = hx_pool.tile([P, LOAD, K], BF16, name="hx_sb")
                 cx_sb[q] = cx_pool.tile([P, LOAD, K], BF16, name="cx_sb")
-            slots = slice(h * PAIR, (h + 1) * PAIR)
-            nc.sync.dma_start(out=hx_sb[q][:, lo : lo + PAIR, :], in_=hx_v[:, slots, :])
-            nc.sync.dma_start(out=cx_sb[q][:, lo : lo + PAIR, :], in_=cx_v[:, slots, :])
-            nc.sync.dma_start(out=xg_sb[q][:, lo : lo + PAIR, :], in_=xg_v[:, slots, :])
+            slots = slice(s0, s0 + count)
+            nc.sync.dma_start(out=hx_sb[q][:, lo : lo + count, :], in_=hx_v[:, slots, :])
+            nc.sync.dma_start(out=cx_sb[q][:, lo : lo + count, :], in_=cx_v[:, slots, :])
+            nc.sync.dma_start(out=xg_sb[q][:, lo : lo + count, :], in_=xg_v[:, slots, :])
+
+        def load_pair(h):
+            load_slots(h * PAIR, PAIR)
 
         emitted = [0]
 
@@ -379,9 +382,10 @@ def tile_ircnn_lstmcell_pa_t_kernel(
                     in_=w_rows[m].rearrange("(u p e) k -> p u (e k)", u=HALVES, e=2),
                 )
 
-        load_pair(0)
+        load_slots(0, 1)
         for m in range(N_WEIGHTS):
             load_w(m)
+        load_slots(1, 1)
 
         neg_b = const.tile([P, 1], F32)
         nc.vector.tensor_scalar(out=neg_b[:], in0=b_bf[:], scalar1=-1.0, scalar2=None, op0=ALU.mult)

from contextlib import ExitStack

import concourse.mybir as mybir
from concourse.masks import make_identity

F32 = mybir.dt.float32
BF16 = mybir.dt.bfloat16
U32 = mybir.dt.uint32
U8 = mybir.dt.uint8
FP8X4 = mybir.dt.float8_e4m3fn_x4
ALU = mybir.AluOpType
ACT = mybir.ActivationFunctionType

P = 128
B = 4096
K = 512
OUT = 512
GATES = 3
IN_GATE, FORGET_GATE, CANDIDATE = 0, 1, 2
PACK = 4
MX_ALIGN = 64
HALVES = 2
SLOTS = B // P
LOAD = 4
PAIR = 2
W_TILES = OUT // P
BANK_TILES = 2
STATES = 2
HX, CX = 0, 1
DECAYS = 2
FORCOFF, INCOFF = 0, 1
HH_I, PEEP_I, HH_G, HH_F, PEEP_F = 0, 1, 2, 3, 4
N_WEIGHTS = 5
TURNED = 2
TILES = 4

LEAD_F = 6
LOAD_AHEAD = 5
FIRST_STEP = -7
W_FIRST_STEP = -5

FLOPS = 2 * B * K * (GATES * OUT + 2 * OUT)


def tile_ircnn_lstmcell_pa_t_kernel(
    tc, xg, hx, cx, td0, td1, w_hh, w_pi, w_pf, b_hh, a, b, out
):
    nc = tc.nc
    with ExitStack() as ctx:
        ctx.enter_context(tc.manual_schedule())

        def pool(name, bufs):
            return ctx.enter_context(tc.tile_pool(name=name, bufs=bufs))

        const = pool("const", 1)
        wraw_pool = pool("wraw", 3)
        wstage = pool("wstage", 2)
        xg_pool = pool("xg", 3)
        hx_pool = pool("hx", 3)
        cx_pool = pool("cx", 4)
        pref_pool = pool("pref", LEAD_F + 1)
        xgt_pool = pool("xgt", 3)
        grouped_pool = pool("grouped", 2)
        packed_pool = pool("packed", 3)
        zt_pool = pool("zt", 3)
        sig_pool = pool("sig", 3)
        p1_pool = pool("p1", 5)
        p2t_pool = pool("p2t", 4)
        store_pool = pool("store", 3)
        psum_tr = ctx.enter_context(tc.psum_pool(name="psum_tr", bufs=2))
        psum_f = ctx.enter_context(tc.psum_pool(name="psum_f", bufs=1))
        psum_z = ctx.enter_context(tc.psum_pool(name="psum_z", bufs=1))
        psum_cx = ctx.enter_context(tc.psum_pool(name="psum_cx", bufs=1))
        psum_o = ctx.enter_context(tc.psum_pool(name="psum_o", bufs=2))

        xg_v = xg.rearrange("(p s) c -> p s c", s=SLOTS)
        hx_v = hx.rearrange("(p s) k -> p s k", s=SLOTS)
        cx_v = cx.rearrange("(p s) k -> p s k", s=SLOTS)
        out_v = out.rearrange("(p s) c -> p s c", s=SLOTS)

        sizes = [1, 1, 2, 2, 2] + [4] * 5 + [2, 1, 1]
        first_of, size_of, grp_of = [], [], {}
        for size in sizes:
            start = sum(size_of)
            for i in range(size):
                grp_of[start + i] = len(first_of)
            first_of.append(start)
            size_of.append(size)
        assert sum(size_of) == SLOTS

        def tr_step(s):
            if s < 1:
                return FIRST_STEP
            return max(s - size_of[grp_of[s]] - 2, (s - 2) // 2)

        def q_step(g):
            return tr_step(first_of[g] + size_of[g] - 1) + 1

        def out_step(s):
            g = grp_of[s]
            return s + size_of[g] + 1

        xg_sb, hx_sb, cx_sb, xgt_sb, grouped_sb, codes_sb, scales_sb = {}, {}, {}, {}, {}, {}, {}
        pref_sb, bankf_ps, bankz_ps, zt_sb, sig_sb, cx_ps, p1_sb, p2t_sb, banko_ps = (
            {}, {}, {}, {}, {}, {}, {}, {}, {},
        )
        pending = []

        def load_slots(s0, count):
            q, lo = divmod(s0, LOAD)
            if lo == 0:
                xg_sb[q] = xg_pool.tile([P, LOAD, GATES * OUT], BF16, name="xg_sb")
                hx_sb[q] = hx_pool.tile([P, LOAD, K], BF16, name="hx_sb")
                cx_sb[q] = cx_pool.tile([P, LOAD, K], BF16, name="cx_sb")
            slots = slice(s0, s0 + count)
            nc.sync.dma_start(out=hx_sb[q][:, lo : lo + count, :], in_=hx_v[:, slots, :])
            nc.sync.dma_start(out=cx_sb[q][:, lo : lo + count, :], in_=cx_v[:, slots, :])
            nc.sync.dma_start(out=xg_sb[q][:, lo : lo + count, :], in_=xg_v[:, slots, :])

        def load_pair(h):
            load_slots(h * PAIR, PAIR)

        emitted = [0]

        def flush(keep=0):
            while len(pending) - emitted[0] > keep:
                pending[emitted[0]]()
                emitted[0] += 1

        def new_tr_bank(shape):
            flush(keep=1)
            return psum_tr.tile(shape, F32, name="tr")

        def transpose_words(dst, words):
            nc.tensor.transpose(dst, words, ident[:])

        def stage_turn_state(s):
            q, place = divmod(s, LOAD)
            g = grp_of[s]
            j = s - first_of[g]
            tr = new_tr_bank([P, STATES, HALVES, P])
            for o, src in ((HX, hx_sb[q]), (CX, cx_sb[q])):
                words = src[:, place, :].bitcast(F32)
                for u in range(HALVES):
                    transpose_words(tr[:, o, u, :], words[:, u * P : (u + 1) * P])
            if j == 0:
                grouped_sb[g] = grouped_pool.tile(
                    [P, STATES, size_of[g], P, PACK], BF16, align_bytes=MX_ALIGN, name="grouped"
                )
            dst = grouped_sb[g][:, :, j].bitcast(F32)
            pending.append(
                lambda: nc.scalar.copy(out=dst, in_=tr[:].rearrange("p o u r -> p o r u"))
            )

        def stage_turn_xg(s):
            q, place = divmod(s, LOAD)
            g = grp_of[s]
            j = s - first_of[g]
            tr = new_tr_bank([P, TURNED, HALVES, P])
            words = xg_sb[q][:, place, :].bitcast(F32)
            for y, gate in enumerate((IN_GATE, CANDIDATE)):
                for u in range(HALVES):
                    w0 = gate * (OUT // 2) + u * P
                    transpose_words(tr[:, y, u, :], words[:, w0 : w0 + P])
            if j == 0:
                xgt_sb[g] = xgt_pool.tile([P, size_of[g], TURNED, HALVES, P], F32, name="xgt")
            dst = xgt_sb[g][:, j]
            pending.append(lambda: nc.scalar.copy(out=dst, in_=tr[:]))

        def stage_quantise(g):
            size = size_of[g]
            codes_sb[g] = packed_pool.tile([P, STATES, size, P], U32, align_bytes=MX_ALIGN, name="codes")
            scales_sb[g] = packed_pool.tile([P, STATES, size, P], U8, align_bytes=MX_ALIGN, name="scales")
            nc.vector.quantize_mx(
                out=codes_sb[g][:].rearrange("p o i r -> p (o i r)").bitcast(FP8X4),
                scales=scales_sb[g][:].rearrange("p o i r -> p (o i r)"),
                in_=grouped_sb[g][:].rearrange("p o i r t -> p (o i r t)"),
            )

        def stage_bias_f(s):
            q, place = divmod(s, LOAD)
            pref_sb[s] = pref_pool.tile([P, OUT], F32, name="pref")
            nc.gpsimd.tensor_tensor(
                out=pref_sb[s][:],
                in0=xg_sb[q][:, place, FORGET_GATE * OUT : (FORGET_GATE + 1) * OUT],
                in1=bias_f_sb[:],
                op=ALU.add,
            )

        def stage_matmul_f(s):
            g = grp_of[s]
            j = s - first_of[g]
            bank_f = psum_f.tile([P, OUT], F32)
            for state, m in ((HX, HH_F), (CX, PEEP_F)):
                nc.tensor.matmul_mx(
                    out=bank_f[:],
                    lhsT=codes_sb[g][:, state, j, :].bitcast(FP8X4),
                    lhsT_scale=scales_sb[g][:, state, j, :],
                    rhs=w_codes[:, m, :].bitcast(FP8X4),
                    rhs_scale=w_scales[:, m, :],
                    start=(state == HX),
                    stop=(state == CX),
                )
            bankf_ps[s] = bank_f

        def stage_sum_f(s):
            nc.vector.tensor_tensor(
                out=pref_sb[s][:], in0=bankf_ps[s][:], in1=pref_sb[s][:], op=ALU.add
            )

        def stage_sigmoid_f(s):
            sig_sb[s] = sig_pool.tile([P, OUT], F32, name="sig")
            nc.scalar.activation(out=sig_sb[s][:], in_=pref_sb[s][:], func=ACT.Sigmoid)

        def stage_cx_psum(s):
            q, place = divmod(s, LOAD)
            cx_ps[s] = psum_cx.tile([P, OUT], F32, name="cx_ps")
            nc.tensor.matmul(
                out=cx_ps[s][:], lhsT=ident_bf[:], rhs=cx_sb[q][:, place, :], start=True, stop=True
            )

        def stage_p1(s):
            p1_sb[s] = p1_pool.tile([P, OUT], F32, name="p1")
            nc.vector.scalar_tensor_tensor(
                out=p1_sb[s][:],
                in0=sig_sb[s][:],
                scalar=decay[:, FORCOFF, s : s + 1],
                in1=cx_ps[s][:],
                op0=ALU.mult,
                op1=ALU.mult,
            )

        def tiles_of(s):
            g = grp_of[s]
            share = TILES // size_of[g]
            j = s - first_of[g]
            return list(range(j * share, (j + 1) * share))

        def stage_matmul_t(s, y):
            g = grp_of[s]
            width = size_of[g] * P
            if y == 0:
                bank_zi = psum_z.tile([P, OUT], F32)
                bank = bank_zi
                passes = ((HX, HH_I), (CX, PEEP_I))
            else:
                bank_zg = psum_z.tile([P, OUT], F32)
                bank = bank_zg
                passes = ((HX, HH_G),)
            for i, tile_no in enumerate(tiles_of(s)):
                for state, m in passes:
                    nc.tensor.matmul_mx(
                        out=bank[:, i * width : (i + 1) * width],
                        lhsT=w_codes[:, m, tile_no * P : (tile_no + 1) * P].bitcast(FP8X4),
                        lhsT_scale=w_scales[:, m, tile_no * P : (tile_no + 1) * P],
                        rhs=codes_sb[g][:, state].rearrange("p i r -> p (i r)").bitcast(FP8X4),
                        rhs_scale=scales_sb[g][:, state].rearrange("p i r -> p (i r)"),
                        start=(state == passes[0][0]),
                        stop=(state == passes[-1][0]),
                    )
            bankz_ps[(s, y)] = bank

        def shaped(ap, size):
            if size == 4:
                return ap.rearrange("p (i r) -> p i r", i=4)
            if size == 2:
                return ap.rearrange("p (e i r) -> p e i r", e=2, i=2)
            return ap.rearrange("p (u e r) -> p u e r", u=2, e=2)

        def xg_turned(s, y):
            g = grp_of[s]
            size = size_of[g]
            flat = xgt_sb[g][:].rearrange("p i y u r -> p (i y u r)").bitcast(BF16)
            v = flat.rearrange("p (i y u r e) -> p i y u r e", i=size, y=TURNED, u=HALVES, e=2)
            first_tile = tiles_of(s)[0]
            if size == 4:
                return v[:, :, y, first_tile // 2, :, first_tile % 2]
            if size == 2:
                return v[:, :, y, first_tile // 2, :, :].rearrange("p i r e -> p e i r")
            return v[:, 0, y].rearrange("p u r e -> p u e r")

        def stage_sum_t(s, y):
            size = size_of[grp_of[s]]
            zt_sb[(s, y)] = zt_pool.tile([P, OUT], F32, name="zt%d" % y)
            nc.vector.tensor_tensor(
                out=shaped(zt_sb[(s, y)][:], size),
                in0=shaped(bankz_ps[(s, y)][:], size),
                in1=xg_turned(s, y),
                op=ALU.add,
            )

        def stage_act_t(s, y):
            width = size_of[grp_of[s]] * P
            for i, tile_no in enumerate(tiles_of(s)):
                part = zt_sb[(s, y)][:, i * width : (i + 1) * width]
                nc.scalar.activation(
                    out=part,
                    in_=part,
                    func=(ACT.Sigmoid if y == 0 else ACT.Tanh),
                    bias=bias_col[:, y, tile_no : tile_no + 1],
                )

        def stage_p2t(s):
            g = grp_of[s]
            j = s - first_of[g]
            if j == 0:
                p2t_sb[g] = p2t_pool.tile([P, TILES * size_of[g] * P], F32, name="p2t")
            nc.gpsimd.tensor_tensor(
                out=p2t_sb[g][:, j * OUT : (j + 1) * OUT],
                in0=zt_sb[(s, 0)][:],
                in1=zt_sb[(s, 1)][:],
                op=ALU.mult,
            )

        def stage_turn_back(s):
            g = grp_of[s]
            j = s - first_of[g]
            width = size_of[g] * P
            banko_ps[s] = psum_o.tile([P, 2, HALVES, P], F32, name="bank_o")
            for tile_no in range(TILES):
                c0 = tile_no * width + j * P
                nc.tensor.transpose(
                    banko_ps[s][:, tile_no % 2, tile_no // 2, :], p2t_sb[g][:, c0 : c0 + P], ident[:]
                )

        def stage_final(s):
            out_sb = store_pool.tile([P, OUT], F32)
            nc.vector.scalar_tensor_tensor(
                out=out_sb[:].rearrange("r (w e) -> r w e", e=2),
                in0=banko_ps[s][:].rearrange("r e u p -> r (u p) e"),
                scalar=decay[:, INCOFF, s : s + 1],
                in1=p1_sb[s][:].rearrange("r (w e) -> r w e", e=2),
                op0=ALU.mult,
                op1=ALU.add,
            )
            nc.sync.dma_start(out=out_v[:, s, :], in_=out_sb[:])

        bias_row = const.tile([P, OUT], BF16)
        nc.vector.memset(bias_row[:], 0.0)
        nc.scalar.dma_start(
            out=bias_row[0:1, :],
            in_=b_hh[FORGET_GATE * OUT : (FORGET_GATE + 1) * OUT].rearrange("(x n) -> x n", x=1),
        )
        a_bf = const.tile([P, 1], BF16)
        nc.scalar.dma_start(out=a_bf[:], in_=a.partition_broadcast(P))
        b_bf = const.tile([P, 1], BF16)
        nc.scalar.dma_start(out=b_bf[:], in_=b.partition_broadcast(P))
        td_bf = const.tile([P, DECAYS, SLOTS], BF16)
        nc.scalar.dma_start(out=td_bf[:, FORCOFF, :], in_=td0.rearrange("(p s) -> p s", s=SLOTS))
        nc.scalar.dma_start(out=td_bf[:, INCOFF, :], in_=td1.rearrange("(p s) -> p s", s=SLOTS))
        bias_col_bf = {}
        for y, gate in enumerate((IN_GATE, CANDIDATE)):
            bias_col_bf[y] = const.tile([P, HALVES, 2], BF16, name="bias_col_bf%d" % y)
            nc.scalar.dma_start(
                out=bias_col_bf[y][:],
                in_=b_hh[gate * OUT : (gate + 1) * OUT].rearrange("(u p e) -> p u e", u=HALVES, e=2),
            )
        ones = const.tile([P, P], BF16)
        nc.vector.memset(ones[:], 1.0)
        ident = const.tile([P, P], F32)
        make_identity(nc, ident[:])
        ident_bf = const.tile([P, P], BF16)
        make_identity(nc, ident_bf[:])

        w_hh_g = w_hh.rearrange("(g n) k -> g n k", g=GATES)
        w_rows = {
            HH_I: w_hh_g[IN_GATE],
            PEEP_I: w_pi,
            HH_G: w_hh_g[CANDIDATE],
            HH_F: w_hh_g[FORGET_GATE],
            PEEP_F: w_pf,
        }
        w_raw = {}

        def load_w(m):
            w_raw[m] = wraw_pool.tile([P, W_TILES, K], BF16, name="w_raw")
            if m in (HH_F, PEEP_F):
                nc.sync.dma_start(out=w_raw[m][:], in_=w_rows[m].rearrange("(j p) k -> p j k", p=P))
            else:
                nc.sync.dma_start(
                    out=w_raw[m][:].rearrange("p (u e) k -> p u (e k)", e=2),
                    in_=w_rows[m].rearrange("(u p e) k -> p u (e k)", u=HALVES, e=2),
                )

        load_slots(0, 1)
        for m in range(N_WEIGHTS):
            load_w(m)
        load_slots(1, 1)

        neg_b = const.tile([P, 1], F32)
        nc.vector.tensor_scalar(out=neg_b[:], in0=b_bf[:], scalar1=-1.0, scalar2=None, op0=ALU.mult)
        a_f32 = const.tile([P, 1], F32)
        nc.vector.tensor_copy(out=a_f32[:], in_=a_bf[:])
        decay_exp = const.tile([P, DECAYS, SLOTS], F32)
        nc.scalar.activation(out=decay_exp[:], in_=td_bf[:], func=ACT.Exp, scale=neg_b[:, 0:1])
        decay = const.tile([P, DECAYS, SLOTS], F32)
        nc.vector.tensor_scalar(
            out=decay[:], in0=decay_exp[:], scalar1=a_f32[:, 0:1], scalar2=None, op0=ALU.mult
        )
        table_warmer = const.tile([P, 1], F32)
        nc.scalar.activation(out=table_warmer[:], in_=neg_b[:], func=ACT.Sigmoid)
        bias_col = const.tile([P, TURNED, TILES], F32)
        for y in range(TURNED):
            nc.vector.tensor_copy(
                out=bias_col[:, y, :], in_=bias_col_bf[y][:].rearrange("p u e -> p (u e)")
            )

        bank_f = psum_f.tile([P, OUT], F32)
        nc.tensor.matmul(out=bank_f[:], lhsT=ones[:], rhs=bias_row[:], start=True, stop=True)
        bias_f_sb = const.tile([P, OUT], F32)
        nc.scalar.copy(out=bias_f_sb[:], in_=bank_f[:])

        w_codes = const.tile([P, N_WEIGHTS, OUT], U32, align_bytes=MX_ALIGN)
        w_scales = const.tile([P, N_WEIGHTS, OUT], U8, align_bytes=MX_ALIGN)

        def stage_weight(m):
            w_grouped = wstage.tile([P, OUT, PACK], BF16, align_bytes=MX_ALIGN)
            w_grouped_words = w_grouped[:].bitcast(F32)
            for part in range(W_TILES // BANK_TILES):
                tr = new_tr_bank([P, BANK_TILES, HALVES, P])
                for j in range(BANK_TILES):
                    words = w_raw[m][:, BANK_TILES * part + j, :].bitcast(F32)
                    for u in range(HALVES):
                        transpose_words(tr[:, j, u, :], words[:, u * P : (u + 1) * P])
                cols = slice(BANK_TILES * part * P, BANK_TILES * (part + 1) * P)
                dst = w_grouped_words[:, cols, :].rearrange("p (j n) u -> p j n u", j=BANK_TILES)
                src = tr[:].rearrange("p j u n -> p j n u")
                if part == 0:
                    nc.scalar.copy(out=dst, in_=src)
                else:
                    nc.vector.tensor_copy(out=dst, in_=src)
            nc.vector.quantize_mx(
                out=w_codes[:, m, :].bitcast(FP8X4),
                scales=w_scales[:, m, :],
                in_=w_grouped[:].rearrange("p n t -> p (n t)"),
            )

        def due(s):
            return 0 <= s < SLOTS

        for step in range(FIRST_STEP, SLOTS + 6):
            flush()
            for h in range(1, SLOTS // PAIR):
                if max(tr_step(h * PAIR) - LOAD_AHEAD, FIRST_STEP) == step:
                    load_pair(h)
            if 0 <= step - W_FIRST_STEP < N_WEIGHTS:
                stage_weight(step - W_FIRST_STEP)
            outs = [s for s in range(SLOTS) if out_step(s) == step]
            for s in outs[:2]:
                stage_turn_back(s)
            if due(step):
                stage_sum_f(step)
                stage_sigmoid_f(step)
                stage_sum_t(step, 0)
                stage_act_t(step, 0)
            if due(step - 1):
                stage_p1(step - 1)
            if due(step):
                stage_sum_t(step, 1)
                stage_act_t(step, 1)
            for i, s in enumerate(outs):
                if i >= 2:
                    stage_turn_back(s)
                stage_final(s)
            for g in range(len(first_of)):
                if q_step(g) == step:
                    stage_quantise(g)
            turns = [s for s in range(SLOTS) if tr_step(s) == step]
            for s in turns:
                stage_turn_state(s)
            if due(step + 1):
                stage_matmul_f(step + 1)
                stage_matmul_t(step + 1, 0)
            for s in turns:
                stage_turn_xg(s)
            if due(step):
                stage_cx_psum(step)
            if due(step + 1):
                stage_matmul_t(step + 1, 1)
            if due(step):
                stage_p2t(step)
            for s in range(SLOTS):
                if max(s - LEAD_F, tr_step(s)) == step:
                    stage_bias_f(s)
